import numpy as np
import ml_dtypes


def mxq(x, axis, fmt="e4m3"):
    dtype, down = {"e4m3": (ml_dtypes.float8_e4m3fn, 7), "e5m2": (ml_dtypes.float8_e5m2, 14)}[fmt]
    v = np.moveaxis(np.asarray(x, np.float32).astype(ml_dtypes.bfloat16).astype(np.float64), axis, -1)
    blocks = v.reshape(v.shape[:-1] + (-1, 32))
    amax = np.abs(blocks).max(-1, keepdims=True)
    byte = np.maximum(np.where(amax > 0, np.frexp(amax)[1] - 1 + 127, 0) - down, 1)
    scale = np.exp2(byte - 127.0)
    codes = (blocks / scale).astype(np.float32).astype(dtype).astype(np.float64)
    return np.moveaxis((codes * scale).reshape(v.shape), -1, axis)


WIDE = False


def mx_kscale(k):
    if not WIDE:
        return np.ones(k)
    levels = np.array([10, -10, 5, -5, 0])
    if k % 512:
        return np.exp2(np.random.permutation(np.resize(levels, k // 32))).repeat(32)
    a = np.empty((k // 512, 16))
    for p in range(k // 512):
        a[p, :8] = np.random.permutation(np.resize(levels, 8))
        for g in range(8):
            far = levels[np.abs(levels - a[p, g]) >= 10]
            a[p, g + 8] = far[np.random.randint(len(far))]
    return np.exp2(a.ravel()).repeat(32)


BF16 = ml_dtypes.bfloat16


def bf(x):
    return np.asarray(x, np.float32).astype(BF16)


def f64(x):
    return np.asarray(x).astype(np.float64)


B, N, E, H, C = 1, 1024, 2048, 8, 512
D = E // H
THETA_SCALE = 1.0e4


def position_thetas():
    return np.repeat(1.0 / THETA_SCALE ** np.linspace(0.0, 1.0, D // 2), 2)


def multiply_by_i(t):
    return np.stack((-t[..., 1::2], t[..., ::2]), axis=-1).reshape(t.shape)


def draw0():
    s = mx_kscale(E)
    return {"x": bf(np.random.standard_normal((B, N, E)) * s),
            "w": bf(np.random.standard_normal((E, E)) / np.sqrt(E) / s[:, None]),
            "b": bf(np.random.standard_normal(E) * 0.3)}


def core(x, w, b):
    p = (mxq(f64(x), 2, "e4m3") @ mxq(f64(w), 0, "e4m3")) + f64(b)
    p = p.reshape(B, N, H, D).transpose(0, 2, 1, 3)
    pos = f64(np.arange(N))[:, None] * position_thetas()[None, :]
    return p * np.cos(pos)[None, None] + multiply_by_i(p) * np.sin(pos)[None, None]


def e4m3fn_bytes(y):
    return np.clip(np.asarray(y, np.float64), -448.0, 448.0).astype(np.float32).astype(ml_dtypes.float8_e4m3fn).view(np.uint8)


def e4m3fn_values(b):
    return np.asarray(b, np.uint8).view(ml_dtypes.float8_e4m3fn).astype(np.float64)


def setup_inputs():
    d = draw0()
    x0 = np.asarray(d['w']).astype(np.float64)
    s = (np.max(np.abs(x0), axis=(1,), keepdims=True) / 448.0).astype(np.float32)
    out = {}
    for k, v in d.items():
        if k == 'w':
            out['w_bytes'] = e4m3fn_bytes(x0 / s.astype(np.float64))
            out['w_scale'] = s
        else:
            out[k] = v
    return out


def reference(x, w_bytes, w_scale, b):
    return core(x, e4m3fn_values(w_bytes) * w_scale.astype(np.float64), b)

@@ -1,0 +1,383 @@
+from contextlib import ExitStack
+
+import concourse.mybir as mybir
+from concourse.masks import make_identity
+
+F32 = mybir.dt.float32
+BF16 = mybir.dt.bfloat16
+I32 = mybir.dt.int32
+U32 = mybir.dt.uint32
+U8 = mybir.dt.uint8
+FP8 = mybir.dt.float8_e4m3fn
+FP8X4 = mybir.dt.float8_e4m3fn_x4
+ALU = mybir.AluOpType
+ACT = mybir.ActivationFunctionType
+
+P = 128
+N_TOK = 1024
+E = 2048
+H = 8
+FLOPS = 2 * N_TOK * E * E
+
+Q = 10000.0 ** (-1.0 / 127.0)
+PI = 3.141592653589793
+TWO_PI = 2.0 * PI
+C1 = 51472.0 / 8192.0
+C2 = TWO_PI - C1
+INT2 = "VVVVVSSS"
+
+
+def tile_multiscaleretention_pa_kernel(tc, x, w_bytes, w_scale, b, out):
+    nc = tc.nc
+    with ExitStack() as ctx:
+        const = ctx.enter_context(tc.tile_pool(name="const", bufs=1))
+        xin = ctx.enter_context(tc.tile_pool(name="xin", bufs=1))
+        wbp = ctx.enter_context(tc.tile_pool(name="wbp", bufs=1))
+        scr = ctx.enter_context(tc.tile_pool(name="scr", bufs=1))
+        wprep = ctx.enter_context(tc.tile_pool(name="wprep", bufs=2))
+        wq = ctx.enter_context(tc.tile_pool(name="wq", bufs=3))
+        xprep = ctx.enter_context(tc.tile_pool(name="xprep", bufs=4))
+        epi = ctx.enter_context(tc.tile_pool(name="epi", bufs=2))
+        outp = ctx.enter_context(tc.tile_pool(name="outp", bufs=3))
+        psa = ctx.enter_context(tc.psum_pool(name="psa", bufs=2))
+        pst = ctx.enter_context(tc.psum_pool(name="pst", bufs=4))
+        ctx.enter_context(tc.manual_schedule())
+
+        zero = const.tile([P, 1], F32, name="zero")
+        nc.vector.memset(zero[:], 0.0)
+        warm = const.tile([P, 1], F32, name="warm")
+        nc.scalar.activation(out=warm[:], in_=zero[:], func=ACT.Sin)
+        halfpi = const.tile([P, 1], F32, name="halfpi")
+        nc.vector.tensor_scalar(out=halfpi[:], in0=zero[:], scalar1=1.0, scalar2=PI / 2.0,
+                                op0=ALU.mult, op1=ALU.add)
+
+        wsc = const.tile([P, 4, 4], F32, name="wsc")
+        nc.scalar.dma_start(out=wsc[:], in_=w_scale.rearrange("(g p t) o -> p g (t o)", p=P, t=4))
+        b16 = const.tile([P, H, 2], BF16, name="b16")
+        nc.scalar.dma_start(out=b16[:], in_=b.rearrange("(h j e) -> j h e", h=H, e=2))
+
+        wsrc = {}
+
+        def load_w(h0, heads):
+            width = 256 * heads
+            for g in range(4):
+                wbt = wbp.tile([P, 4, width], U8, name="wb%d_%d" % (h0, g))
+                nc.sync.dma_start(
+                    out=wbt[:],
+                    in_=w_bytes[512 * g:512 * (g + 1), 256 * h0:256 * h0 + width].rearrange("(p t) n -> p t n", t=4))
+                for hh in range(heads):
+                    wsrc[(h0 + hh, g)] = (wbt, 256 * hh)
+
+        x_sb = []
+
+        def load_x(nh):
+            xt = xin.tile([P, 4, 2048], BF16, name="xin%d" % nh)
+            xv = x[0, 512 * nh:512 * (nh + 1), :].rearrange("(p i) k -> p i k", i=4)
+            for ip in range(2):
+                nc.sync.dma_start(out=xt[:, 2 * ip:2 * ip + 2, :], in_=xv[:, 2 * ip:2 * ip + 2, :])
+            x_sb.append(xt)
+
+        load_w(0, 1)
+        load_x(0)
+        load_w(1, 1)
+        load_x(1)
+        load_w(2, 2)
+        load_w(4, 2)
+        load_w(6, 2)
+
+        jcol = const.tile([P, 7], I32, name="jcol")
+        nc.gpsimd.iota(jcol[:], pattern=[[0, 7]], base=0, channel_multiplier=1)
+        shf = const.tile([P, 7], I32, name="shf")
+        nc.gpsimd.iota(shf[:], pattern=[[1, 7]], base=0, channel_multiplier=0)
+        nfb = const.tile([P, 132], F32, name="nfb")
+        nc.gpsimd.iota(nfb[:, 0:128], pattern=[[4, 128]], base=0, channel_multiplier=0,
+                       allow_small_or_imprecise_dtypes=True)
+        nc.gpsimd.iota(nfb[:, 128:132], pattern=[[511, 2], [1, 2]], base=1, channel_multiplier=0,
+                       allow_small_or_imprecise_dtypes=True)
+        ident = const.tile([P, P], F32, name="ident")
+        make_identity(nc, ident[:])
+
+        bits = const.tile([P, 7], I32, name="bits")
+        nc.vector.tensor_tensor(out=bits[:], in0=jcol[:], in1=shf[:], op=ALU.logical_shift_right)
+        bit1 = const.tile([P, 7], I32, name="bit1")
+        nc.vector.tensor_scalar(out=bit1[:], in0=bits[:], scalar1=1, scalar2=None, op0=ALU.bitwise_and)
+        nbit = const.tile([P, 7], F32, name="nbit")
+        nc.vector.tensor_scalar(out=nbit[:], in0=bit1[:], scalar1=-1.0, scalar2=1.0, op0=ALU.mult, op1=ALU.add)
+        fac = const.tile([P, 7], F32, name="fac")
+        for bb in range(7):
+            nc.vector.tensor_scalar(out=fac[:, bb:bb + 1], in0=nbit[:, bb:bb + 1],
+                                    scalar1=Q ** (2 ** bb), scalar2=None, op0=ALU.max)
+        pr3 = const.tile([P, 3], F32, name="pr3")
+        nc.vector.tensor_tensor(out=pr3[:], in0=fac[:, 0:3], in1=fac[:, 3:6], op=ALU.mult)
+        pr2 = const.tile([P, 2], F32, name="pr2")
+        nc.vector.tensor_tensor(out=pr2[:, 0:1], in0=pr3[:, 0:1], in1=pr3[:, 1:2], op=ALU.mult)
+        nc.vector.tensor_tensor(out=pr2[:, 1:2], in0=pr3[:, 2:3], in1=fac[:, 6:7], op=ALU.mult)
+        theta = const.tile([P, 1], F32, name="theta")
+        nc.vector.tensor_tensor(out=theta[:], in0=pr2[:, 0:1], in1=pr2[:, 1:2], op=ALU.mult)
+
+        cosT = const.tile([P, N_TOK], F32, name="cosT")
+        sinT = const.tile([P, N_TOK], F32, name="sinT")
+        cx = const.tile([P, 4], F32, name="cx")
+        sx = const.tile([P, 4], F32, name="sx")
+        sn = scr.tile([P, 132], F32, name="sn")
+        cs = scr.tile([P, 132], F32, name="cs")
+
+        def base_args():
+            kk = scr.tile([P, 132], I32, name="kk")
+            nc.vector.tensor_scalar(out=kk[:], in0=nfb[:], scalar1=theta[:, 0:1], scalar2=1.0 / TWO_PI,
+                                    op0=ALU.mult, op1=ALU.mult)
+            kf = scr.tile([P, 132], F32, name="kf")
+            nc.vector.tensor_copy(out=kf[:], in_=kk[:])
+            kc1 = scr.tile([P, 132], F32, name="kc1")
+            nc.vector.tensor_scalar(out=kc1[:], in0=kf[:], scalar1=C1, scalar2=None, op0=ALU.mult)
+            r1 = scr.tile([P, 132], F32, name="r1")
+            nc.vector.scalar_tensor_tensor(out=r1[:], in0=nfb[:], scalar=theta[:, 0:1], in1=kc1[:],
+                                           op0=ALU.mult, op1=ALU.subtract)
+            rr = scr.tile([P, 132], F32, name="rr")
+            nc.vector.scalar_tensor_tensor(out=rr[:], in0=kf[:], scalar=-C2, in1=r1[:],
+                                           op0=ALU.mult, op1=ALU.add)
+            psi = scr.tile([P, 132], F32, name="psi")
+            nc.vector.tensor_scalar(out=psi[:], in0=rr[:], scalar1=0.5, scalar2=-PI / 4.0,
+                                    op0=ALU.mult, op1=ALU.add)
+            ab = scr.tile([P, 132], F32, name="ab")
+            nc.vector.scalar_tensor_tensor(out=ab[:], in0=psi[:], scalar=-1.0, in1=psi[:],
+                                           op0=ALU.mult, op1=ALU.max)
+            nc.scalar.activation(out=sn[:], in_=psi[:], func=ACT.Sin)
+            nc.scalar.activation(out=cs[:], in_=ab[:], func=ACT.Sin, scale=-1.0, bias=halfpi[:, 0:1])
+
+        def base_tables():
+            tmp = scr.tile([P, 132], F32, name="tmp")
+            nc.vector.scalar_tensor_tensor(out=tmp[:], in0=sn[:], scalar=-2.0, in1=sn[:],
+                                           op0=ALU.mult, op1=ALU.mult)
+            for dst_c, dst_s, cols in ((cx[:], sx[:], slice(128, 132)), (cosT[:, 0:128], sinT[:, 0:128], slice(0, 128))):
+                nc.vector.scalar_tensor_tensor(out=dst_c, in0=sn[:, cols], scalar=-2.0, in1=cs[:, cols],
+                                               op0=ALU.mult, op1=ALU.mult)
+                nc.vector.tensor_scalar(out=dst_s, in0=tmp[:, cols], scalar1=1.0, scalar2=1.0,
+                                        op0=ALU.mult, op1=ALU.add)
+
+        def rotate(width, k, which):
+            src = slice(0, width)
+            dst = slice(width, 2 * width)
+            t1 = scr.tile([P, 512], F32, name="rot%d" % which)
+            if which == 0:
+                nc.vector.tensor_scalar(out=t1[:, src], in0=sinT[:, src], scalar1=sx[:, k:k + 1], scalar2=None,
+                                        op0=ALU.mult)
+                nc.vector.scalar_tensor_tensor(out=cosT[:, dst], in0=cosT[:, src], scalar=cx[:, k:k + 1],
+                                               in1=t1[:, src], op0=ALU.mult, op1=ALU.subtract)
+            else:
+                nc.vector.tensor_scalar(out=t1[:, src], in0=cosT[:, src], scalar1=sx[:, k:k + 1], scalar2=None,
+                                        op0=ALU.mult)
+                nc.vector.scalar_tensor_tensor(out=sinT[:, dst], in0=sinT[:, src], scalar=cx[:, k:k + 1],
+                                               in1=t1[:, src], op0=ALU.mult, op1=ALU.add)
+
+        xc = [const.tile([P, 4, 512], U32, name="xc%d" % nh, align_bytes=64) for nh in range(2)]
+        xs = [const.tile([P, 4, 512], U8, name="xs%d" % nh, align_bytes=64) for nh in range(2)]
+        xg = {}
+        xbank = {}
+
+        def x_tr(nh, g, ip):
+            xt = pst.tile([P, 2, 2, P], F32, name="tr")
+            for i2 in range(2):
+                words = x_sb[nh][:, 2 * ip + i2, :].bitcast(F32)
+                for u in range(2):
+                    nc.tensor.transpose(xt[:, i2, u, :], words[:, 256 * g + u:256 * (g + 1):2], ident[:])
+            xbank[(nh, g, ip)] = xt
+
+        def x_ev(nh, g, ip, eng):
+            if (nh, g) not in xg:
+                xg[(nh, g)] = xprep.tile([P, 2048], BF16, name="xg", align_bytes=64)
+            xgw = xg[(nh, g)][:].bitcast(F32)
+            dst = xgw[:, 512 * ip:512 * (ip + 1)].rearrange("p (i r u) -> p i r u", i=2, u=2)
+            src = xbank[(nh, g, ip)][:].rearrange("p i u r -> p i r u")
+            if eng == "V":
+                nc.vector.tensor_copy(out=dst, in_=src)
+            else:
+                nc.scalar.copy(out=dst, in_=src)
+
+        def x_q(nh, g):
+            nc.vector.quantize_mx(out=xc[nh][:, g, :].bitcast(FP8X4), scales=xs[nh][:, g, :], in_=xg[(nh, g)][:])
+
+        deq = {}
+        grp = {}
+        wc = {}
+        ws = {}
+
+        def w_deq(h, g, eng="S"):
+            if h not in deq:
+                deq[h] = wprep.tile([P, 16, 256], BF16, name="deq")
+            wbt, c0 = wsrc[(h, g)]
+            for t in range(4):
+                if eng == "S":
+                    nc.scalar.activation(out=deq[h][:, 4 * g + t, :], in_=wbt[:, t, c0:c0 + 256].bitcast(FP8),
+                                         func=ACT.Copy, scale=wsc[:, g, t:t + 1])
+                else:
+                    nc.vector.tensor_scalar(out=deq[h][:, 4 * g + t, :], in0=wbt[:, t, c0:c0 + 256].bitcast(FP8),
+                                            scalar1=wsc[:, g, t:t + 1], scalar2=None, op0=ALU.mult)
+
+        def w_int(h, g, eng):
+            if h not in grp:
+                grp[h] = wprep.tile([P, 4096], BF16, name="grp", align_bytes=64)
+            dst = grp[h][:, 1024 * g:1024 * (g + 1)].rearrange("p (e j t) -> p e j t", e=2, t=4)
+            src = deq[h][:, 4 * g:4 * g + 4, :].rearrange("p t (j e) -> p e j t", e=2)
+            if eng == "S":
+                nc.scalar.copy(out=dst, in_=src)
+            else:
+                nc.vector.tensor_copy(out=dst, in_=src)
+
+        def w_q(h, g0, ng):
+            if h not in wc:
+                wc[h] = wq.tile([P, 1024], U32, name="wcod", align_bytes=64)
+                ws[h] = wq.tile([P, 1024], U8, name="wsca", align_bytes=64)
+            nc.vector.quantize_mx(out=wc[h][:, 256 * g0:256 * (g0 + ng)].bitcast(FP8X4),
+                                  scales=ws[h][:, 256 * g0:256 * (g0 + ng)],
+                                  in_=grp[h][:, 1024 * g0:1024 * (g0 + ng)])
+
+        acc = {}
+        prod = {}
+        trb = {}
+        bias = const.tile([P, 2 * H], F32, name="bias")
+
+        def mx(u):
+            h, nh = u // 2, u % 2
+            acc[u] = []
+            for e in range(2):
+                a = psa.tile([P, 512], F32, name="acc%d" % e)
+                for g in range(4):
+                    wcols = slice(256 * g + 128 * e, 256 * g + 128 * (e + 1))
+                    nc.tensor.matmul_mx(out=a[:], lhsT=wc[h][:, wcols].bitcast(FP8X4), lhsT_scale=ws[h][:, wcols],
+                                        rhs=xc[nh][:, g, :].bitcast(FP8X4), rhs_scale=xs[nh][:, g, :],
+                                        start=(g == 0), stop=(g == 3))
+                acc[u].append(a)
+
+        def products(u):
+            h, nh = u // 2, u % 2
+            cols = slice(512 * nh, 512 * (nh + 1))
+            be = bias[:, 2 * h:2 * h + 1]
+            bo = bias[:, 2 * h + 1:2 * h + 2]
+            u1 = epi.tile([P, 512], F32, name="u1")
+            u2 = epi.tile([P, 512], F32, name="u2")
+            u3 = epi.tile([P, 512], F32, name="u3")
+            u4 = epi.tile([P, 512], F32, name="u4")
+            nc.vector.scalar_tensor_tensor(out=u1[:], in0=acc[u][0][:], scalar=be, in1=cosT[:, cols],
+                                           op0=ALU.add, op1=ALU.mult)
+            nc.vector.scalar_tensor_tensor(out=u2[:], in0=acc[u][1][:], scalar=bo, in1=sinT[:, cols],
+                                           op0=ALU.add, op1=ALU.mult)
+            o0 = epi.tile([P, 512], F32, name="o0")
+            nc.gpsimd.tensor_tensor(out=o0[:], in0=u1[:], in1=u2[:], op=ALU.subtract)
+            nc.vector.scalar_tensor_tensor(out=u3[:], in0=acc[u][1][:], scalar=bo, in1=cosT[:, cols],
+                                           op0=ALU.add, op1=ALU.mult)
+            nc.vector.scalar_tensor_tensor(out=u4[:], in0=acc[u][0][:], scalar=be, in1=sinT[:, cols],
+                                           op0=ALU.add, op1=ALU.mult)
+            prod[u] = [[o0], [u3, u4]]
+
+        def back(u):
+            trb[u] = []
+            for ip in range(2):
+                tr = pst.tile([P, 2, 2, P], F32, name="tr")
+                for i2 in range(2):
+                    blk = slice(128 * (2 * ip + i2), 128 * (2 * ip + i2 + 1))
+                    for e in range(2):
+                        parts = prod[u][e]
+                        for q, part in enumerate(parts):
+                            nc.tensor.matmul(out=tr[:, i2, e, :], lhsT=part[:, blk], rhs=ident[:], is_transpose=True,
+                                             start=(q == 0), stop=(q == len(parts) - 1))
+                trb[u].append(tr)
+
+        def leave(u, engs="SS"):
+            h, nh = u // 2, u % 2
+            osb = outp.tile([P, 4, 256], F32, name="osb")
+            dram = out[0, h, 512 * nh:512 * (nh + 1), :].rearrange("(p i) d -> p i d", i=4)
+            for ip in range(2):
+                dst = osb[:, 2 * ip:2 * ip + 2, :].rearrange("p i (j e) -> p i j e", e=2)
+                src = trb[u][ip][:].rearrange("p i e j -> p i j e")
+                if engs[ip] == "S":
+                    nc.scalar.copy(out=dst, in_=src)
+                else:
+                    nc.vector.tensor_copy(out=dst, in_=src)
+                if u == 2 * H - 1:
+                    nc.sync.dma_start(out=dram[:, 2 * ip:2 * ip + 2, :], in_=osb[:, 2 * ip:2 * ip + 2, :])
+            if u != 2 * H - 1:
+                nc.sync.dma_start(out=dram, in_=osb[:])
+
+        base_args()
+        for g in range(4):
+            w_deq(0, g)
+        base_tables()
+        rotate(128, 0, 0)
+        rotate(128, 0, 1)
+        w_int(0, 0, "V")
+        rotate(256, 1, 0)
+        w_int(0, 1, "V")
+        rotate(256, 1, 1)
+        for g in range(4):
+            x_tr(0, g, 0)
+        w_int(0, 2, "V")
+        x_ev(0, 0, 0, "V")
+        x_ev(0, 1, 0, "V")
+        x_ev(0, 2, 0, "S")
+        x_ev(0, 3, 0, "S")
+        for g in range(4):
+            x_tr(0, g, 1)
+        w_int(0, 3, "V")
+        w_q(0, 0, 4)
+        nc.vector.tensor_copy(out=bias[:], in_=b16[:].rearrange("p h e -> p (h e)"))
+        x_ev(0, 0, 1, "V")
+        x_ev(0, 1, 1, "S")
+        x_q(0, 0)
+        x_ev(0, 2, 1, "V")
+        x_ev(0, 3, 1, "S")
+        x_q(0, 1)
+        x_q(0, 2)
+        x_q(0, 3)
+        mx(0)
+        w_deq(1, 0)
+        w_deq(1, 1)
+        for g in range(4):
+            x_tr(1, g, 0)
+        w_deq(1, 2)
+        w_deq(1, 3)
+        w_int(1, 0, "V")
+        w_int(1, 1, "V")
+        products(0)
+        for g in range(4):
+            x_ev(1, g, 0, "S")
+        for g in range(4):
+            x_tr(1, g, 1)
+        w_int(1, 2, "V")
+        w_int(1, 3, "V")
+        for g in range(4):
+            x_ev(1, g, 1, "SV"[g % 2])
+            x_q(1, g)
+        mx(1)
+        back(0)
+        w_q(1, 0, 4)
+        rotate(512, 2, 0)
+        rotate(512, 2, 1)
+        w_deq(2, 0)
+        w_deq(2, 1)
+        mx(2)
+        products(1)
+        leave(0)
+        w_deq(2, 2)
+        w_deq(2, 3)
+
+        for u in range(2, 2 * H):
+            h, half = u // 2, u % 2
+            back(u - 1)
+            if h + 1 < H:
+                if half == 0:
+                    w_int(h + 1, 0, "V")
+                    w_int(h + 1, 1, "V")
+                    w_int(h + 1, 2, INT2[h + 1])
+                    w_int(h + 1, 3, "S")
+                else:
+                    w_q(h + 1, 0, 4)
+            if u + 1 < 2 * H:
+                mx(u + 1)
+            if h + 2 < H:
+                w_deq(h + 2, 2 * half)
+                w_deq(h + 2, 2 * half + 1)
+            products(u)
+            leave(u - 1)
+        back(2 * H - 1)
+        leave(2 * H - 1, "SV")

@@ -24,7 +24,6 @@ PI = 3.141592653589793
 TWO_PI = 2.0 * PI
 C1 = 51472.0 / 8192.0
 C2 = TWO_PI - C1
-INT2 = "VVVVVSSS"
 
 
 def tile_multiscaleretention_pa_kernel(tc, x, w_bytes, w_scale, b, out):
@@ -39,6 +38,7 @@ def tile_multiscaleretention_pa_kernel(tc, x, w_bytes, w_scale, b, out):
         xprep = ctx.enter_context(tc.tile_pool(name="xprep", bufs=4))
         epi = ctx.enter_context(tc.tile_pool(name="epi", bufs=2))
         outp = ctx.enter_context(tc.tile_pool(name="outp", bufs=3))
+        tokp = ctx.enter_context(tc.tile_pool(name="tokp", bufs=3))
         psa = ctx.enter_context(tc.psum_pool(name="psa", bufs=2))
         pst = ctx.enter_context(tc.psum_pool(name="pst", bufs=4))
         ctx.enter_context(tc.manual_schedule())
@@ -117,6 +117,12 @@ def tile_multiscaleretention_pa_kernel(tc, x, w_bytes, w_scale, b, out):
 
         cosT = const.tile([P, N_TOK], F32, name="cosT")
         sinT = const.tile([P, N_TOK], F32, name="sinT")
+        nsinT = const.tile([P, N_TOK], F32, name="nsinT")
+
+        def negate(nh):
+            cols = slice(512 * nh, 512 * (nh + 1))
+            nc.scalar.activation(out=nsinT[:, cols], in_=sinT[:, cols], func=ACT.Copy, scale=-1.0)
+
         cx = const.tile([P, 4], F32, name="cx")
         sx = const.tile([P, 4], F32, name="sx")
         sn = scr.tile([P, 132], F32, name="sn")
@@ -142,6 +148,9 @@ def tile_multiscaleretention_pa_kernel(tc, x, w_bytes, w_scale, b, out):
             ab = scr.tile([P, 132], F32, name="ab")
             nc.vector.scalar_tensor_tensor(out=ab[:], in0=psi[:], scalar=-1.0, in1=psi[:],
                                            op0=ALU.mult, op1=ALU.max)
+            return psi, ab
+
+        def base_sines(psi, ab):
             nc.scalar.activation(out=sn[:], in_=psi[:], func=ACT.Sin)
             nc.scalar.activation(out=cs[:], in_=ab[:], func=ACT.Sin, scale=-1.0, bias=halfpi[:, 0:1])
 
@@ -221,8 +230,18 @@ def tile_multiscaleretention_pa_kernel(tc, x, w_bytes, w_scale, b, out):
             src = deq[h][:, 4 * g:4 * g + 4, :].rearrange("p t (j e) -> p e j t", e=2)
             if eng == "S":
                 nc.scalar.copy(out=dst, in_=src)
-            else:
+            elif eng == "V":
                 nc.vector.tensor_copy(out=dst, in_=src)
+            else:
+                nc.gpsimd.tensor_scalar(out=dst, in0=src, scalar1=token[0][:, 0:1], scalar2=0.0,
+                                        op0=ALU.mult, op1=ALU.add)
+
+        token = [None]
+
+        def new_token():
+            tok = tokp.tile([P, 1], F32, name="tok")
+            nc.vector.tensor_scalar(out=tok[:], in0=zero[:], scalar1=1.0, scalar2=1.0, op0=ALU.mult, op1=ALU.add)
+            token[0] = tok
 
         def w_q(h, g0, ng):
             if h not in wc:
@@ -249,135 +268,139 @@ def tile_multiscaleretention_pa_kernel(tc, x, w_bytes, w_scale, b, out):
                                         start=(g == 0), stop=(g == 3))
                 acc[u].append(a)
 
-        def products(u):
+        def products(u, pieces=1):
             h, nh = u // 2, u % 2
-            cols = slice(512 * nh, 512 * (nh + 1))
             be = bias[:, 2 * h:2 * h + 1]
             bo = bias[:, 2 * h + 1:2 * h + 2]
             u1 = epi.tile([P, 512], F32, name="u1")
             u2 = epi.tile([P, 512], F32, name="u2")
             u3 = epi.tile([P, 512], F32, name="u3")
             u4 = epi.tile([P, 512], F32, name="u4")
-            nc.vector.scalar_tensor_tensor(out=u1[:], in0=acc[u][0][:], scalar=be, in1=cosT[:, cols],
-                                           op0=ALU.add, op1=ALU.mult)
-            nc.vector.scalar_tensor_tensor(out=u2[:], in0=acc[u][1][:], scalar=bo, in1=sinT[:, cols],
-                                           op0=ALU.add, op1=ALU.mult)
-            o0 = epi.tile([P, 512], F32, name="o0")
-            nc.gpsimd.tensor_tensor(out=o0[:], in0=u1[:], in1=u2[:], op=ALU.subtract)
-            nc.vector.scalar_tensor_tensor(out=u3[:], in0=acc[u][1][:], scalar=bo, in1=cosT[:, cols],
-                                           op0=ALU.add, op1=ALU.mult)
-            nc.vector.scalar_tensor_tensor(out=u4[:], in0=acc[u][0][:], scalar=be, in1=sinT[:, cols],
-                                           op0=ALU.add, op1=ALU.mult)
-            prod[u] = [[o0], [u3, u4]]
+            prod[u] = [[u1, u2], [u3, u4]]
+            width = 512 // pieces
+            for piece in range(pieces):
+                c = slice(width * piece, width * (piece + 1))
+                tcols = slice(512 * nh + width * piece, 512 * nh + width * (piece + 1))
+                for dst, e, table in ((u1, 0, cosT), (u2, 1, nsinT), (u3, 1, cosT), (u4, 0, sinT)):
+                    nc.vector.scalar_tensor_tensor(out=dst[:, c], in0=acc[u][e][:, c], scalar=(be, bo)[e],
+                                                   in1=table[:, tcols], op0=ALU.add, op1=ALU.mult)
+                if pieces > 1:
+                    back(u, (piece,))
 
-        def back(u):
-            trb[u] = []
-            for ip in range(2):
+        def back(u, ips=(0, 1)):
+            for ip in ips:
                 tr = pst.tile([P, 2, 2, P], F32, name="tr")
                 for i2 in range(2):
                     blk = slice(128 * (2 * ip + i2), 128 * (2 * ip + i2 + 1))
                     for e in range(2):
-                        parts = prod[u][e]
-                        for q, part in enumerate(parts):
+                        for q, part in enumerate(prod[u][e]):
                             nc.tensor.matmul(out=tr[:, i2, e, :], lhsT=part[:, blk], rhs=ident[:], is_transpose=True,
-                                             start=(q == 0), stop=(q == len(parts) - 1))
-                trb[u].append(tr)
+                                             start=(q == 0), stop=(q == 1))
+                trb[(u, ip)] = tr
 
-        def leave(u, engs="SS"):
+        def leave(u, engs="SS", stores=1):
             h, nh = u // 2, u % 2
             osb = outp.tile([P, 4, 256], F32, name="osb")
             dram = out[0, h, 512 * nh:512 * (nh + 1), :].rearrange("(p i) d -> p i d", i=4)
             for ip in range(2):
                 dst = osb[:, 2 * ip:2 * ip + 2, :].rearrange("p i (j e) -> p i j e", e=2)
-                src = trb[u][ip][:].rearrange("p i e j -> p i j e")
+                src = trb[(u, ip)][:].rearrange("p i e j -> p i j e")
                 if engs[ip] == "S":
                     nc.scalar.copy(out=dst, in_=src)
                 else:
                     nc.vector.tensor_copy(out=dst, in_=src)
-                if u == 2 * H - 1:
+                if stores == 2:
                     nc.sync.dma_start(out=dram[:, 2 * ip:2 * ip + 2, :], in_=osb[:, 2 * ip:2 * ip + 2, :])
-            if u != 2 * H - 1:
+            if stores == 1:
                 nc.sync.dma_start(out=dram, in_=osb[:])
 
-        base_args()
-        for g in range(4):
-            w_deq(0, g)
+        psi_ab = base_args()
+        w_deq(0, 0)
+        w_deq(0, 1)
+        base_sines(psi_ab[0], psi_ab[1])
+        w_deq(0, 2)
+        w_deq(0, 3)
+        w_int(0, 0, "V")
+        w_int(0, 1, "V")
         base_tables()
         rotate(128, 0, 0)
         rotate(128, 0, 1)
-        w_int(0, 0, "V")
-        rotate(256, 1, 0)
-        w_int(0, 1, "V")
-        rotate(256, 1, 1)
+        w_int(0, 2, "V")
         for g in range(4):
             x_tr(0, g, 0)
-        w_int(0, 2, "V")
         x_ev(0, 0, 0, "V")
-        x_ev(0, 1, 0, "V")
+        x_ev(0, 1, 0, "S")
         x_ev(0, 2, 0, "S")
         x_ev(0, 3, 0, "S")
         for g in range(4):
             x_tr(0, g, 1)
         w_int(0, 3, "V")
         w_q(0, 0, 4)
-        nc.vector.tensor_copy(out=bias[:], in_=b16[:].rearrange("p h e -> p (h e)"))
         x_ev(0, 0, 1, "V")
         x_ev(0, 1, 1, "S")
-        x_q(0, 0)
-        x_ev(0, 2, 1, "V")
+        x_ev(0, 2, 1, "S")
         x_ev(0, 3, 1, "S")
-        x_q(0, 1)
-        x_q(0, 2)
-        x_q(0, 3)
+        for g in range(4):
+            x_q(0, g)
         mx(0)
+        rotate(256, 1, 0)
+        rotate(256, 1, 1)
+        nc.vector.tensor_copy(out=bias[:], in_=b16[:].rearrange("p h e -> p (h e)"))
         w_deq(1, 0)
         w_deq(1, 1)
-        for g in range(4):
-            x_tr(1, g, 0)
+        negate(0)
         w_deq(1, 2)
         w_deq(1, 3)
-        w_int(1, 0, "V")
-        w_int(1, 1, "V")
-        products(0)
         for g in range(4):
-            x_ev(1, g, 0, "S")
+            x_tr(1, g, 0)
+        new_token()
+        w_int(1, 0, "G")
+        w_int(1, 1, "G")
+        products(0)
+        x_ev(1, 0, 0, "V")
+        x_ev(1, 1, 0, "V")
+        x_ev(1, 2, 0, "S")
+        x_ev(1, 3, 0, "S")
         for g in range(4):
             x_tr(1, g, 1)
         w_int(1, 2, "V")
         w_int(1, 3, "V")
+        w_q(1, 0, 4)
         for g in range(4):
-            x_ev(1, g, 1, "SV"[g % 2])
+            x_ev(1, g, 1, "S")
+        for g in range(4):
             x_q(1, g)
         mx(1)
         back(0)
-        w_q(1, 0, 4)
+        mx(2)
         rotate(512, 2, 0)
         rotate(512, 2, 1)
         w_deq(2, 0)
         w_deq(2, 1)
-        mx(2)
-        products(1)
-        leave(0)
+        negate(1)
         w_deq(2, 2)
         w_deq(2, 3)
+        w_int(2, 1, "V")
+        new_token()
+        w_int(2, 0, "G")
+        products(1)
+        leave(0)
 
         for u in range(2, 2 * H):
             h, half = u // 2, u % 2
             back(u - 1)
-            if h + 1 < H:
-                if half == 0:
-                    w_int(h + 1, 0, "V")
-                    w_int(h + 1, 1, "V")
-                    w_int(h + 1, 2, INT2[h + 1])
-                    w_int(h + 1, 3, "S")
-                else:
-                    w_q(h + 1, 0, 4)
+            if half == 1 and h + 1 < H:
+                w_q(h + 1, 0, 4)
             if u + 1 < 2 * H:
                 mx(u + 1)
             if h + 2 < H:
                 w_deq(h + 2, 2 * half)
                 w_deq(h + 2, 2 * half + 1)
-            products(u)
+            k = h + 1 + half
+            if k < H:
+                w_int(k, 3 - 2 * half, "V")
+                new_token()
+                w_int(k, 2 - 2 * half, "G")
+            products(u, 2 if u == 2 * H - 1 else 1)
             leave(u - 1)
-        back(2 * H - 1)
-        leave(2 * H - 1, "SV")
+        leave(2 * H - 1, "SV", 2)

@@ -54,7 +54,6 @@ def tile_multiscaleretention_pa_kernel(tc, x, w_bytes, w_scale, b, out):
         wsc = const.tile([P, 4, 4], F32, name="wsc")
         nc.scalar.dma_start(out=wsc[:], in_=w_scale.rearrange("(g p t) o -> p g (t o)", p=P, t=4))
         b16 = const.tile([P, H, 2], BF16, name="b16")
-        nc.scalar.dma_start(out=b16[:], in_=b.rearrange("(h j e) -> j h e", h=H, e=2))
 
         wsrc = {}
 
@@ -79,16 +78,15 @@ def tile_multiscaleretention_pa_kernel(tc, x, w_bytes, w_scale, b, out):
 
         load_w(0, 1)
         load_x(0)
+        nc.sync.dma_start(out=b16[:], in_=b.rearrange("(h j e) -> j h e", h=H, e=2))
         load_w(1, 1)
         load_x(1)
         load_w(2, 2)
         load_w(4, 2)
         load_w(6, 2)
 
-        jcol = const.tile([P, 7], I32, name="jcol")
-        nc.gpsimd.iota(jcol[:], pattern=[[0, 7]], base=0, channel_multiplier=1)
-        shf = const.tile([P, 7], I32, name="shf")
-        nc.gpsimd.iota(shf[:], pattern=[[1, 7]], base=0, channel_multiplier=0)
+        jcol = const.tile([P, 1], I32, name="jcol")
+        nc.gpsimd.iota(jcol[:], pattern=[[0, 1]], base=0, channel_multiplier=1)
         nfb = const.tile([P, 132], F32, name="nfb")
         nc.gpsimd.iota(nfb[:, 0:128], pattern=[[4, 128]], base=0, channel_multiplier=0,
                        allow_small_or_imprecise_dtypes=True)
@@ -96,17 +94,17 @@ def tile_multiscaleretention_pa_kernel(tc, x, w_bytes, w_scale, b, out):
                        allow_small_or_imprecise_dtypes=True)
         ident = const.tile([P, P], F32, name="ident")
         make_identity(nc, ident[:])
+        warmt = const.tile([P, 512], BF16, name="warmt")
+        nc.gpsimd.memset(warmt[:], 0.0)
 
-        bits = const.tile([P, 7], I32, name="bits")
-        nc.vector.tensor_tensor(out=bits[:], in0=jcol[:], in1=shf[:], op=ALU.logical_shift_right)
-        bit1 = const.tile([P, 7], I32, name="bit1")
-        nc.vector.tensor_scalar(out=bit1[:], in0=bits[:], scalar1=1, scalar2=None, op0=ALU.bitwise_and)
-        nbit = const.tile([P, 7], F32, name="nbit")
-        nc.vector.tensor_scalar(out=nbit[:], in0=bit1[:], scalar1=-1.0, scalar2=1.0, op0=ALU.mult, op1=ALU.add)
+        bit = const.tile([P, 7], I32, name="bit")
+        for bb in range(7):
+            nc.vector.tensor_scalar(out=bit[:, bb:bb + 1], in0=jcol[:], scalar1=bb, scalar2=1,
+                                    op0=ALU.logical_shift_right, op1=ALU.bitwise_and)
         fac = const.tile([P, 7], F32, name="fac")
         for bb in range(7):
-            nc.vector.tensor_scalar(out=fac[:, bb:bb + 1], in0=nbit[:, bb:bb + 1],
-                                    scalar1=Q ** (2 ** bb), scalar2=None, op0=ALU.max)
+            nc.vector.tensor_scalar(out=fac[:, bb:bb + 1], in0=bit[:, bb:bb + 1], scalar1=0.0, scalar2=Q ** (2 ** bb),
+                                    op0=ALU.is_equal, op1=ALU.max)
         pr3 = const.tile([P, 3], F32, name="pr3")
         nc.vector.tensor_tensor(out=pr3[:], in0=fac[:, 0:3], in1=fac[:, 3:6], op=ALU.mult)
         pr2 = const.tile([P, 2], F32, name="pr2")
@@ -128,56 +126,69 @@ def tile_multiscaleretention_pa_kernel(tc, x, w_bytes, w_scale, b, out):
         sn = scr.tile([P, 132], F32, name="sn")
         cs = scr.tile([P, 132], F32, name="cs")
 
-        def base_args():
-            kk = scr.tile([P, 132], I32, name="kk")
-            nc.vector.tensor_scalar(out=kk[:], in0=nfb[:], scalar1=theta[:, 0:1], scalar2=1.0 / TWO_PI,
-                                    op0=ALU.mult, op1=ALU.mult)
-            kf = scr.tile([P, 132], F32, name="kf")
-            nc.vector.tensor_copy(out=kf[:], in_=kk[:])
-            kc1 = scr.tile([P, 132], F32, name="kc1")
-            nc.vector.tensor_scalar(out=kc1[:], in0=kf[:], scalar1=C1, scalar2=None, op0=ALU.mult)
-            r1 = scr.tile([P, 132], F32, name="r1")
-            nc.vector.scalar_tensor_tensor(out=r1[:], in0=nfb[:], scalar=theta[:, 0:1], in1=kc1[:],
-                                           op0=ALU.mult, op1=ALU.subtract)
-            rr = scr.tile([P, 132], F32, name="rr")
-            nc.vector.scalar_tensor_tensor(out=rr[:], in0=kf[:], scalar=-C2, in1=r1[:],
-                                           op0=ALU.mult, op1=ALU.add)
-            psi = scr.tile([P, 132], F32, name="psi")
-            nc.vector.tensor_scalar(out=psi[:], in0=rr[:], scalar1=0.5, scalar2=-PI / 4.0,
-                                    op0=ALU.mult, op1=ALU.add)
-            ab = scr.tile([P, 132], F32, name="ab")
-            nc.vector.scalar_tensor_tensor(out=ab[:], in0=psi[:], scalar=-1.0, in1=psi[:],
-                                           op0=ALU.mult, op1=ALU.max)
-            return psi, ab
+        kk = scr.tile([P, 132], I32, name="kk")
+        kc1 = scr.tile([P, 132], F32, name="kc1")
+        r1 = scr.tile([P, 132], F32, name="r1")
+        rr = scr.tile([P, 132], F32, name="rr")
+        psi = scr.tile([P, 132], F32, name="psi")
+        ab = scr.tile([P, 132], F32, name="ab")
+        tmp = scr.tile([P, 132], F32, name="tmp")
 
-        def base_sines(psi, ab):
+        def arg_step(step):
+            if step == 0:
+                nc.vector.tensor_scalar(out=kk[:], in0=nfb[:], scalar1=theta[:, 0:1], scalar2=1.0 / TWO_PI,
+                                        op0=ALU.mult, op1=ALU.mult)
+            elif step == 1:
+                nc.vector.tensor_scalar(out=kc1[:], in0=kk[:], scalar1=C1, scalar2=None, op0=ALU.mult)
+            elif step == 2:
+                nc.vector.scalar_tensor_tensor(out=r1[:], in0=nfb[:], scalar=theta[:, 0:1], in1=kc1[:],
+                                               op0=ALU.mult, op1=ALU.subtract)
+            elif step == 3:
+                nc.vector.scalar_tensor_tensor(out=rr[:], in0=kk[:], scalar=-C2, in1=r1[:],
+                                               op0=ALU.mult, op1=ALU.add)
+            elif step == 4:
+                nc.vector.tensor_scalar(out=psi[:], in0=rr[:], scalar1=0.5, scalar2=-PI / 4.0,
+                                        op0=ALU.mult, op1=ALU.add)
+            else:
+                nc.vector.scalar_tensor_tensor(out=ab[:], in0=psi[:], scalar=-1.0, in1=psi[:],
+                                               op0=ALU.mult, op1=ALU.max)
+
+        def base_sines():
             nc.scalar.activation(out=sn[:], in_=psi[:], func=ACT.Sin)
             nc.scalar.activation(out=cs[:], in_=ab[:], func=ACT.Sin, scale=-1.0, bias=halfpi[:, 0:1])
 
-        def base_tables():
-            tmp = scr.tile([P, 132], F32, name="tmp")
-            nc.vector.scalar_tensor_tensor(out=tmp[:], in0=sn[:], scalar=-2.0, in1=sn[:],
-                                           op0=ALU.mult, op1=ALU.mult)
-            for dst_c, dst_s, cols in ((cx[:], sx[:], slice(128, 132)), (cosT[:, 0:128], sinT[:, 0:128], slice(0, 128))):
-                nc.vector.scalar_tensor_tensor(out=dst_c, in0=sn[:, cols], scalar=-2.0, in1=cs[:, cols],
+        def base_step(step):
+            if step == 0:
+                nc.vector.scalar_tensor_tensor(out=tmp[:], in0=sn[:], scalar=-2.0, in1=sn[:],
                                                op0=ALU.mult, op1=ALU.mult)
-                nc.vector.tensor_scalar(out=dst_s, in0=tmp[:, cols], scalar1=1.0, scalar2=1.0,
+            elif step == 1:
+                nc.vector.scalar_tensor_tensor(out=cx[:], in0=sn[:, 128:132], scalar=-2.0, in1=cs[:, 128:132],
+                                               op0=ALU.mult, op1=ALU.mult)
+                nc.vector.scalar_tensor_tensor(out=cosT[:, 0:128], in0=sn[:, 0:128], scalar=-2.0, in1=cs[:, 0:128],
+                                               op0=ALU.mult, op1=ALU.mult)
+            else:
+                nc.vector.tensor_scalar(out=sx[:], in0=tmp[:, 128:132], scalar1=1.0, scalar2=1.0,
+                                        op0=ALU.mult, op1=ALU.add)
+                nc.vector.tensor_scalar(out=sinT[:, 0:128], in0=tmp[:, 0:128], scalar1=1.0, scalar2=1.0,
                                         op0=ALU.mult, op1=ALU.add)
 
-        def rotate(width, k, which):
+        rot = {}
+
+        def rotate_a(width, k):
+            src = slice(0, width)
+            for which, table in ((0, sinT), (1, cosT)):
+                t1 = scr.tile([P, 512], F32, name="rot%d" % which)
+                nc.vector.tensor_scalar(out=t1[:, src], in0=table[:, src], scalar1=sx[:, k:k + 1], scalar2=None,
+                                        op0=ALU.mult)
+                rot[which] = t1
+
+        def rotate_b(width, k):
             src = slice(0, width)
             dst = slice(width, 2 * width)
-            t1 = scr.tile([P, 512], F32, name="rot%d" % which)
-            if which == 0:
-                nc.vector.tensor_scalar(out=t1[:, src], in0=sinT[:, src], scalar1=sx[:, k:k + 1], scalar2=None,
-                                        op0=ALU.mult)
-                nc.vector.scalar_tensor_tensor(out=cosT[:, dst], in0=cosT[:, src], scalar=cx[:, k:k + 1],
-                                               in1=t1[:, src], op0=ALU.mult, op1=ALU.subtract)
-            else:
-                nc.vector.tensor_scalar(out=t1[:, src], in0=cosT[:, src], scalar1=sx[:, k:k + 1], scalar2=None,
-                                        op0=ALU.mult)
-                nc.vector.scalar_tensor_tensor(out=sinT[:, dst], in0=sinT[:, src], scalar=cx[:, k:k + 1],
-                                               in1=t1[:, src], op0=ALU.mult, op1=ALU.add)
+            nc.vector.scalar_tensor_tensor(out=cosT[:, dst], in0=cosT[:, src], scalar=cx[:, k:k + 1],
+                                           in1=rot[0][:, src], op0=ALU.mult, op1=ALU.subtract)
+            nc.vector.scalar_tensor_tensor(out=sinT[:, dst], in0=sinT[:, src], scalar=cx[:, k:k + 1],
+                                           in1=rot[1][:, src], op0=ALU.mult, op1=ALU.add)
 
         xc = [const.tile([P, 4, 512], U32, name="xc%d" % nh, align_bytes=64) for nh in range(2)]
         xs = [const.tile([P, 4, 512], U8, name="xs%d" % nh, align_bytes=64) for nh in range(2)]
@@ -256,17 +267,25 @@ def tile_multiscaleretention_pa_kernel(tc, x, w_bytes, w_scale, b, out):
         trb = {}
         bias = const.tile([P, 2 * H], F32, name="bias")
 
+        def banks(u):
+            acc[u] = [psa.tile([P, 512], F32, name="acc%d" % e) for e in range(2)]
+
+        def warm(u, count, rhs=None):
+            for q in range(count):
+                nc.tensor.matmul(out=acc[u][0][:], lhsT=warmt[:, 0:P], rhs=(warmt[:] if rhs is None else rhs),
+                                 start=True, stop=True)
+
         def mx(u):
             h, nh = u // 2, u % 2
-            acc[u] = []
+            if u not in acc:
+                banks(u)
             for e in range(2):
-                a = psa.tile([P, 512], F32, name="acc%d" % e)
+                a = acc[u][e]
                 for g in range(4):
                     wcols = slice(256 * g + 128 * e, 256 * g + 128 * (e + 1))
                     nc.tensor.matmul_mx(out=a[:], lhsT=wc[h][:, wcols].bitcast(FP8X4), lhsT_scale=ws[h][:, wcols],
                                         rhs=xc[nh][:, g, :].bitcast(FP8X4), rhs_scale=xs[nh][:, g, :],
                                         start=(g == 0), stop=(g == 3))
-                acc[u].append(a)
 
         def products(u, pieces=1):
             h, nh = u // 2, u % 2
@@ -314,45 +333,59 @@ def tile_multiscaleretention_pa_kernel(tc, x, w_bytes, w_scale, b, out):
             if stores == 1:
                 nc.sync.dma_start(out=dram, in_=osb[:])
 
-        psi_ab = base_args()
+        arg_step(0)
+        arg_step(1)
         w_deq(0, 0)
+        banks(0)
+        warm(0, 1, deq[0][:, 0:2, :].rearrange("p a c -> p (a c)"))
+        warm(0, 5)
         w_deq(0, 1)
-        base_sines(psi_ab[0], psi_ab[1])
         w_deq(0, 2)
-        w_deq(0, 3)
         w_int(0, 0, "V")
+        arg_step(2)
+        arg_step(3)
         w_int(0, 1, "V")
-        base_tables()
-        rotate(128, 0, 0)
-        rotate(128, 0, 1)
+        arg_step(4)
+        arg_step(5)
+        base_sines()
+        w_deq(0, 3)
         w_int(0, 2, "V")
         for g in range(4):
             x_tr(0, g, 0)
+            warm(0, g % 2)
+        base_step(0)
         x_ev(0, 0, 0, "V")
+        base_step(1)
+        base_step(2)
         x_ev(0, 1, 0, "S")
         x_ev(0, 2, 0, "S")
         x_ev(0, 3, 0, "S")
         for g in range(4):
             x_tr(0, g, 1)
+            warm(0, g % 2)
         w_int(0, 3, "V")
+        rotate_a(128, 0)
+        rotate_b(128, 0)
         w_q(0, 0, 4)
-        x_ev(0, 0, 1, "V")
-        x_ev(0, 1, 1, "S")
-        x_ev(0, 2, 1, "S")
-        x_ev(0, 3, 1, "S")
         for g in range(4):
-            x_q(0, g)
+            x_ev(0, g, 1, "S")
+        rotate_a(256, 1)
+        x_q(0, 0)
+        rotate_b(256, 1)
+        x_q(0, 1)
+        x_q(0, 2)
+        x_q(0, 3)
         mx(0)
-        rotate(256, 1, 0)
-        rotate(256, 1, 1)
         nc.vector.tensor_copy(out=bias[:], in_=b16[:].rearrange("p h e -> p (h e)"))
         w_deq(1, 0)
         w_deq(1, 1)
         negate(0)
         w_deq(1, 2)
         w_deq(1, 3)
+        banks(1)
         for g in range(4):
             x_tr(1, g, 0)
+            warm(1, g % 2)
         new_token()
         w_int(1, 0, "G")
         w_int(1, 1, "G")
@@ -363,18 +396,19 @@ def tile_multiscaleretention_pa_kernel(tc, x, w_bytes, w_scale, b, out):
         x_ev(1, 3, 0, "S")
         for g in range(4):
             x_tr(1, g, 1)
+            warm(1, g % 2)
         w_int(1, 2, "V")
         w_int(1, 3, "V")
-        w_q(1, 0, 4)
         for g in range(4):
             x_ev(1, g, 1, "S")
         for g in range(4):
             x_q(1, g)
         mx(1)
+        rotate_a(512, 2)
+        w_q(1, 0, 4)
+        rotate_b(512, 2)
         back(0)
         mx(2)
-        rotate(512, 2, 0)
-        rotate(512, 2, 1)
         w_deq(2, 0)
         w_deq(2, 1)
         negate(1)

@@ -94,8 +94,6 @@ def tile_multiscaleretention_pa_kernel(tc, x, w_bytes, w_scale, b, out):
                        allow_small_or_imprecise_dtypes=True)
         ident = const.tile([P, P], F32, name="ident")
         make_identity(nc, ident[:])
-        warmt = const.tile([P, 512], BF16, name="warmt")
-        nc.gpsimd.memset(warmt[:], 0.0)
 
         bit = const.tile([P, 7], I32, name="bit")
         for bb in range(7):
@@ -270,11 +268,6 @@ def tile_multiscaleretention_pa_kernel(tc, x, w_bytes, w_scale, b, out):
         def banks(u):
             acc[u] = [psa.tile([P, 512], F32, name="acc%d" % e) for e in range(2)]
 
-        def warm(u, count, rhs=None):
-            for q in range(count):
-                nc.tensor.matmul(out=acc[u][0][:], lhsT=warmt[:, 0:P], rhs=(warmt[:] if rhs is None else rhs),
-                                 start=True, stop=True)
-
         def mx(u):
             h, nh = u // 2, u % 2
             if u not in acc:
@@ -336,9 +329,6 @@ def tile_multiscaleretention_pa_kernel(tc, x, w_bytes, w_scale, b, out):
         arg_step(0)
         arg_step(1)
         w_deq(0, 0)
-        banks(0)
-        warm(0, 1, deq[0][:, 0:2, :].rearrange("p a c -> p (a c)"))
-        warm(0, 5)
         w_deq(0, 1)
         w_deq(0, 2)
         w_int(0, 0, "V")
@@ -352,7 +342,6 @@ def tile_multiscaleretention_pa_kernel(tc, x, w_bytes, w_scale, b, out):
         w_int(0, 2, "V")
         for g in range(4):
             x_tr(0, g, 0)
-            warm(0, g % 2)
         base_step(0)
         x_ev(0, 0, 0, "V")
         base_step(1)
@@ -362,7 +351,6 @@ def tile_multiscaleretention_pa_kernel(tc, x, w_bytes, w_scale, b, out):
         x_ev(0, 3, 0, "S")
         for g in range(4):
             x_tr(0, g, 1)
-            warm(0, g % 2)
         w_int(0, 3, "V")
         rotate_a(128, 0)
         rotate_b(128, 0)
@@ -382,10 +370,8 @@ def tile_multiscaleretention_pa_kernel(tc, x, w_bytes, w_scale, b, out):
         negate(0)
         w_deq(1, 2)
         w_deq(1, 3)
-        banks(1)
         for g in range(4):
             x_tr(1, g, 0)
-            warm(1, g % 2)
         new_token()
         w_int(1, 0, "G")
         w_int(1, 1, "G")
@@ -396,7 +382,6 @@ def tile_multiscaleretention_pa_kernel(tc, x, w_bytes, w_scale, b, out):
         x_ev(1, 3, 0, "S")
         for g in range(4):
             x_tr(1, g, 1)
-            warm(1, g % 2)
         w_int(1, 2, "V")
         w_int(1, 3, "V")
         for g in range(4):

@@ -111,13 +111,12 @@ def tile_multiscaleretention_pa_kernel(tc, x, w_bytes, w_scale, b, out):
         theta = const.tile([P, 1], F32, name="theta")
         nc.vector.tensor_tensor(out=theta[:], in0=pr2[:, 0:1], in1=pr2[:, 1:2], op=ALU.mult)
 
-        cosT = const.tile([P, N_TOK], F32, name="cosT")
-        sinT = const.tile([P, N_TOK], F32, name="sinT")
-        nsinT = const.tile([P, N_TOK], F32, name="nsinT")
+        tab_e = const.tile([P, 2, 2, 512], F32, name="tab_e")
+        tab_o = const.tile([P, 2, 2, 512], F32, name="tab_o")
 
-        def negate(nh):
-            cols = slice(512 * nh, 512 * (nh + 1))
-            nc.scalar.activation(out=nsinT[:, cols], in_=sinT[:, cols], func=ACT.Copy, scale=-1.0)
+        def odd_tables(nh):
+            nc.scalar.activation(out=tab_o[:, nh, 0, :], in_=tab_e[:, nh, 1, :], func=ACT.Copy, scale=-1.0)
+            nc.scalar.copy(out=tab_o[:, nh, 1, :], in_=tab_e[:, nh, 0, :])
 
         cx = const.tile([P, 4], F32, name="cx")
         sx = const.tile([P, 4], F32, name="sx")
@@ -162,31 +161,28 @@ def tile_multiscaleretention_pa_kernel(tc, x, w_bytes, w_scale, b, out):
             elif step == 1:
                 nc.vector.scalar_tensor_tensor(out=cx[:], in0=sn[:, 128:132], scalar=-2.0, in1=cs[:, 128:132],
                                                op0=ALU.mult, op1=ALU.mult)
-                nc.vector.scalar_tensor_tensor(out=cosT[:, 0:128], in0=sn[:, 0:128], scalar=-2.0, in1=cs[:, 0:128],
+                nc.vector.scalar_tensor_tensor(out=tab_e[:, 0, 0, 0:128], in0=sn[:, 0:128], scalar=-2.0, in1=cs[:, 0:128],
                                                op0=ALU.mult, op1=ALU.mult)
             else:
                 nc.vector.tensor_scalar(out=sx[:], in0=tmp[:, 128:132], scalar1=1.0, scalar2=1.0,
                                         op0=ALU.mult, op1=ALU.add)
-                nc.vector.tensor_scalar(out=sinT[:, 0:128], in0=tmp[:, 0:128], scalar1=1.0, scalar2=1.0,
+                nc.vector.tensor_scalar(out=tab_e[:, 0, 1, 0:128], in0=tmp[:, 0:128], scalar1=1.0, scalar2=1.0,
                                         op0=ALU.mult, op1=ALU.add)
 
         rot = {}
 
         def rotate_a(width, k):
-            src = slice(0, width)
-            for which, table in ((0, sinT), (1, cosT)):
+            for which in range(2):
                 t1 = scr.tile([P, 512], F32, name="rot%d" % which)
-                nc.vector.tensor_scalar(out=t1[:, src], in0=table[:, src], scalar1=sx[:, k:k + 1], scalar2=None,
-                                        op0=ALU.mult)
+                nc.vector.tensor_scalar(out=t1[:, 0:width], in0=tab_e[:, 0, 1 - which, 0:width], scalar1=sx[:, k:k + 1],
+                                        scalar2=None, op0=ALU.mult)
                 rot[which] = t1
 
         def rotate_b(width, k):
-            src = slice(0, width)
-            dst = slice(width, 2 * width)
-            nc.vector.scalar_tensor_tensor(out=cosT[:, dst], in0=cosT[:, src], scalar=cx[:, k:k + 1],
-                                           in1=rot[0][:, src], op0=ALU.mult, op1=ALU.subtract)
-            nc.vector.scalar_tensor_tensor(out=sinT[:, dst], in0=sinT[:, src], scalar=cx[:, k:k + 1],
-                                           in1=rot[1][:, src], op0=ALU.mult, op1=ALU.add)
+            for which, op in ((0, ALU.subtract), (1, ALU.add)):
+                dst = tab_e[:, 1, which, :] if width == 512 else tab_e[:, 0, which, width:2 * width]
+                nc.vector.scalar_tensor_tensor(out=dst, in0=tab_e[:, 0, which, 0:width], scalar=cx[:, k:k + 1],
+                                               in1=rot[which][:, 0:width], op0=ALU.mult, op1=op)
 
         xc = [const.tile([P, 4, 512], U32, name="xc%d" % nh, align_bytes=64) for nh in range(2)]
         xs = [const.tile([P, 4, 512], U8, name="xs%d" % nh, align_bytes=64) for nh in range(2)]
@@ -282,20 +278,17 @@ def tile_multiscaleretention_pa_kernel(tc, x, w_bytes, w_scale, b, out):
 
         def products(u, pieces=1):
             h, nh = u // 2, u % 2
-            be = bias[:, 2 * h:2 * h + 1]
-            bo = bias[:, 2 * h + 1:2 * h + 2]
-            u1 = epi.tile([P, 512], F32, name="u1")
-            u2 = epi.tile([P, 512], F32, name="u2")
-            u3 = epi.tile([P, 512], F32, name="u3")
-            u4 = epi.tile([P, 512], F32, name="u4")
-            prod[u] = [[u1, u2], [u3, u4]]
+            ue = epi.tile([P, 2, 512], F32, name="ue")
+            uo = epi.tile([P, 2, 512], F32, name="uo")
+            prod[u] = [[ue[:, 0, :], uo[:, 0, :]], [uo[:, 1, :], ue[:, 1, :]]]
             width = 512 // pieces
             for piece in range(pieces):
                 c = slice(width * piece, width * (piece + 1))
-                tcols = slice(512 * nh + width * piece, 512 * nh + width * (piece + 1))
-                for dst, e, table in ((u1, 0, cosT), (u2, 1, nsinT), (u3, 1, cosT), (u4, 0, sinT)):
-                    nc.vector.scalar_tensor_tensor(out=dst[:, c], in0=acc[u][e][:, c], scalar=(be, bo)[e],
-                                                   in1=table[:, tcols], op0=ALU.add, op1=ALU.mult)
+                for dst, e, table in ((ue, 0, tab_e), (uo, 1, tab_o)):
+                    nc.vector.scalar_tensor_tensor(out=dst[:, :, c],
+                                                   in0=acc[u][e][:, c].unsqueeze(1).to_broadcast([P, 2, width]),
+                                                   scalar=bias[:, 2 * h + e:2 * h + e + 1], in1=table[:, nh, :, c],
+                                                   op0=ALU.add, op1=ALU.mult)
                 if pieces > 1:
                     back(u, (piece,))
 
@@ -343,7 +336,7 @@ def tile_multiscaleretention_pa_kernel(tc, x, w_bytes, w_scale, b, out):
         for g in range(4):
             x_tr(0, g, 0)
         base_step(0)
-        x_ev(0, 0, 0, "V")
+        x_ev(0, 0, 0, "S")
         base_step(1)
         base_step(2)
         x_ev(0, 1, 0, "S")
@@ -367,7 +360,7 @@ def tile_multiscaleretention_pa_kernel(tc, x, w_bytes, w_scale, b, out):
         nc.vector.tensor_copy(out=bias[:], in_=b16[:].rearrange("p h e -> p (h e)"))
         w_deq(1, 0)
         w_deq(1, 1)
-        negate(0)
+        odd_tables(0)
         w_deq(1, 2)
         w_deq(1, 3)
         for g in range(4):
@@ -396,7 +389,7 @@ def tile_multiscaleretention_pa_kernel(tc, x, w_bytes, w_scale, b, out):
         mx(2)
         w_deq(2, 0)
         w_deq(2, 1)
-        negate(1)
+        odd_tables(1)
         w_deq(2, 2)
         w_deq(2, 3)
         w_int(2, 1, "V")
@@ -407,11 +400,14 @@ def tile_multiscaleretention_pa_kernel(tc, x, w_bytes, w_scale, b, out):
 
         for u in range(2, 2 * H):
             h, half = u // 2, u % 2
-            back(u - 1)
-            if half == 1 and h + 1 < H:
-                w_q(h + 1, 0, 4)
+            if half == 1:
+                back(u - 1)
+                if h + 1 < H:
+                    w_q(h + 1, 0, 4)
             if u + 1 < 2 * H:
                 mx(u + 1)
+            if half == 0:
+                back(u - 1)
             if h + 2 < H:
                 w_deq(h + 2, 2 * half)
                 w_deq(h + 2, 2 * half + 1)

@@ -76,10 +76,9 @@ def tile_multiscaleretention_pa_kernel(tc, x, w_bytes, w_scale, b, out):
                 nc.sync.dma_start(out=xt[:, 2 * ip:2 * ip + 2, :], in_=xv[:, 2 * ip:2 * ip + 2, :])
             x_sb.append(xt)
 
-        load_w(0, 1)
+        load_w(0, 2)
         load_x(0)
         nc.sync.dma_start(out=b16[:], in_=b.rearrange("(h j e) -> j h e", h=H, e=2))
-        load_w(1, 1)
         load_x(1)
         load_w(2, 2)
         load_w(4, 2)
@@ -111,12 +110,7 @@ def tile_multiscaleretention_pa_kernel(tc, x, w_bytes, w_scale, b, out):
         theta = const.tile([P, 1], F32, name="theta")
         nc.vector.tensor_tensor(out=theta[:], in0=pr2[:, 0:1], in1=pr2[:, 1:2], op=ALU.mult)
 
-        tab_e = const.tile([P, 2, 2, 512], F32, name="tab_e")
-        tab_o = const.tile([P, 2, 2, 512], F32, name="tab_o")
-
-        def odd_tables(nh):
-            nc.scalar.activation(out=tab_o[:, nh, 0, :], in_=tab_e[:, nh, 1, :], func=ACT.Copy, scale=-1.0)
-            nc.scalar.copy(out=tab_o[:, nh, 1, :], in_=tab_e[:, nh, 0, :])
+        tab3 = const.tile([P, 2, 3, 512], F32, name="tab3")
 
         cx = const.tile([P, 4], F32, name="cx")
         sx = const.tile([P, 4], F32, name="sx")
@@ -161,28 +155,35 @@ def tile_multiscaleretention_pa_kernel(tc, x, w_bytes, w_scale, b, out):
             elif step == 1:
                 nc.vector.scalar_tensor_tensor(out=cx[:], in0=sn[:, 128:132], scalar=-2.0, in1=cs[:, 128:132],
                                                op0=ALU.mult, op1=ALU.mult)
-                nc.vector.scalar_tensor_tensor(out=tab_e[:, 0, 0, 0:128], in0=sn[:, 0:128], scalar=-2.0, in1=cs[:, 0:128],
+                nc.vector.scalar_tensor_tensor(out=tab3[:, 0, 1, 0:128], in0=sn[:, 0:128], scalar=-2.0, in1=cs[:, 0:128],
                                                op0=ALU.mult, op1=ALU.mult)
             else:
                 nc.vector.tensor_scalar(out=sx[:], in0=tmp[:, 128:132], scalar1=1.0, scalar2=1.0,
                                         op0=ALU.mult, op1=ALU.add)
-                nc.vector.tensor_scalar(out=tab_e[:, 0, 1, 0:128], in0=tmp[:, 0:128], scalar1=1.0, scalar2=1.0,
+                nc.vector.tensor_scalar(out=tab3[:, 0, 2, 0:128], in0=tmp[:, 0:128], scalar1=1.0, scalar2=1.0,
+                                        op0=ALU.mult, op1=ALU.add)
+                nc.vector.tensor_scalar(out=tab3[:, 0, 0, 0:128], in0=tmp[:, 0:128], scalar1=-1.0, scalar2=-1.0,
                                         op0=ALU.mult, op1=ALU.add)
 
         rot = {}
 
         def rotate_a(width, k):
-            for which in range(2):
-                t1 = scr.tile([P, 512], F32, name="rot%d" % which)
-                nc.vector.tensor_scalar(out=t1[:, 0:width], in0=tab_e[:, 0, 1 - which, 0:width], scalar1=sx[:, k:k + 1],
-                                        scalar2=None, op0=ALU.mult)
-                rot[which] = t1
+            t1 = scr.tile([P, 2, 512], F32, name="rot")
+            nc.vector.tensor_scalar(out=t1[:, :, 0:width], in0=tab3[:, 0, 0:2, 0:width], scalar1=sx[:, k:k + 1],
+                                    scalar2=None, op0=ALU.mult)
+            rot[0] = t1
 
         def rotate_b(width, k):
-            for which, op in ((0, ALU.subtract), (1, ALU.add)):
-                dst = tab_e[:, 1, which, :] if width == 512 else tab_e[:, 0, which, width:2 * width]
-                nc.vector.scalar_tensor_tensor(out=dst, in0=tab_e[:, 0, which, 0:width], scalar=cx[:, k:k + 1],
-                                               in1=rot[which][:, 0:width], op0=ALU.mult, op1=op)
+            dst = tab3[:, 1, 1:3, :] if width == 512 else tab3[:, 0, 1:3, width:2 * width]
+            nc.vector.scalar_tensor_tensor(out=dst, in0=tab3[:, 0, 1:3, 0:width], scalar=cx[:, k:k + 1],
+                                           in1=rot[0][:, :, 0:width], op0=ALU.mult, op1=ALU.add)
+
+        def negate(nh, c0, c1, eng):
+            if eng == "S":
+                nc.scalar.activation(out=tab3[:, nh, 0, c0:c1], in_=tab3[:, nh, 2, c0:c1], func=ACT.Copy, scale=-1.0)
+            else:
+                nc.vector.tensor_scalar(out=tab3[:, nh, 0, c0:c1], in0=tab3[:, nh, 2, c0:c1], scalar1=-1.0, scalar2=None,
+                                        op0=ALU.mult)
 
         xc = [const.tile([P, 4, 512], U32, name="xc%d" % nh, align_bytes=64) for nh in range(2)]
         xs = [const.tile([P, 4, 512], U8, name="xs%d" % nh, align_bytes=64) for nh in range(2)]
@@ -284,10 +285,10 @@ def tile_multiscaleretention_pa_kernel(tc, x, w_bytes, w_scale, b, out):
             width = 512 // pieces
             for piece in range(pieces):
                 c = slice(width * piece, width * (piece + 1))
-                for dst, e, table in ((ue, 0, tab_e), (uo, 1, tab_o)):
+                for dst, e, seg in ((ue, 0, 1), (uo, 1, 0)):
                     nc.vector.scalar_tensor_tensor(out=dst[:, :, c],
                                                    in0=acc[u][e][:, c].unsqueeze(1).to_broadcast([P, 2, width]),
-                                                   scalar=bias[:, 2 * h + e:2 * h + e + 1], in1=table[:, nh, :, c],
+                                                   scalar=bias[:, 2 * h + e:2 * h + e + 1], in1=tab3[:, nh, seg:seg + 2, c],
                                                    op0=ALU.add, op1=ALU.mult)
                 if pieces > 1:
                     back(u, (piece,))
@@ -321,7 +322,7 @@ def tile_multiscaleretention_pa_kernel(tc, x, w_bytes, w_scale, b, out):
 
         arg_step(0)
         arg_step(1)
-        w_deq(0, 0)
+        w_deq(0, 0, "V")
         w_deq(0, 1)
         w_deq(0, 2)
         w_int(0, 0, "V")
@@ -348,6 +349,7 @@ def tile_multiscaleretention_pa_kernel(tc, x, w_bytes, w_scale, b, out):
         rotate_a(128, 0)
         rotate_b(128, 0)
         w_q(0, 0, 4)
+        negate(0, 128, 256, "V")
         for g in range(4):
             x_ev(0, g, 1, "S")
         rotate_a(256, 1)
@@ -360,7 +362,7 @@ def tile_multiscaleretention_pa_kernel(tc, x, w_bytes, w_scale, b, out):
         nc.vector.tensor_copy(out=bias[:], in_=b16[:].rearrange("p h e -> p (h e)"))
         w_deq(1, 0)
         w_deq(1, 1)
-        odd_tables(0)
+        negate(0, 256, 512, "S")
         w_deq(1, 2)
         w_deq(1, 3)
         for g in range(4):
@@ -389,7 +391,7 @@ def tile_multiscaleretention_pa_kernel(tc, x, w_bytes, w_scale, b, out):
         mx(2)
         w_deq(2, 0)
         w_deq(2, 1)
-        odd_tables(1)
+        negate(1, 0, 512, "S")
         w_deq(2, 2)
         w_deq(2, 3)
         w_int(2, 1, "V")

@@ -237,7 +237,9 @@ def tile_multiscaleretention_pa_kernel(tc, x, w_bytes, w_scale, b, out):
             if eng == "S":
                 nc.scalar.copy(out=dst, in_=src)
             elif eng == "V":
-                nc.vector.tensor_copy(out=dst, in_=src)
+                nc.vector.tensor_copy(
+                    out=grp[h][:, 1024 * g:1024 * (g + 1)].rearrange("p (e c i t) -> p e c t i", e=2, i=4, t=4),
+                    in_=deq[h][:, 4 * g:4 * g + 4, :].rearrange("p t (c i e) -> p e c t i", i=4, e=2))
             else:
                 nc.gpsimd.tensor_scalar(out=dst, in0=src, scalar1=token[0][:, 0:1], scalar2=0.0,
                                         op0=ALU.mult, op1=ALU.add)

@@ -39,6 +39,7 @@ def tile_multiscaleretention_pa_kernel(tc, x, w_bytes, w_scale, b, out):
         epi = ctx.enter_context(tc.tile_pool(name="epi", bufs=2))
         outp = ctx.enter_context(tc.tile_pool(name="outp", bufs=3))
         tokp = ctx.enter_context(tc.tile_pool(name="tokp", bufs=3))
+        sump = ctx.enter_context(tc.tile_pool(name="sump", bufs=1))
         psa = ctx.enter_context(tc.psum_pool(name="psa", bufs=2))
         pst = ctx.enter_context(tc.psum_pool(name="pst", bufs=4))
         ctx.enter_context(tc.manual_schedule())
@@ -261,6 +262,7 @@ def tile_multiscaleretention_pa_kernel(tc, x, w_bytes, w_scale, b, out):
 
         acc = {}
         prod = {}
+        pair = {}
         trb = {}
         bias = const.tile([P, 2 * H], F32, name="bias")
 
@@ -284,6 +286,7 @@ def tile_multiscaleretention_pa_kernel(tc, x, w_bytes, w_scale, b, out):
             ue = epi.tile([P, 2, 512], F32, name="ue")
             uo = epi.tile([P, 2, 512], F32, name="uo")
             prod[u] = [[ue[:, 0, :], uo[:, 0, :]], [uo[:, 1, :], ue[:, 1, :]]]
+            pair[u] = (ue, uo)
             width = 512 // pieces
             for piece in range(pieces):
                 c = slice(width * piece, width * (piece + 1))
@@ -295,6 +298,11 @@ def tile_multiscaleretention_pa_kernel(tc, x, w_bytes, w_scale, b, out):
                 if pieces > 1:
                     back(u, (piece,))
 
+        def add(u):
+            sm = sump.tile([P, 2, 512], F32, name="sm")
+            nc.gpsimd.tensor_tensor(out=sm[:], in0=pair[u][0][:], in1=pair[u][1][:], op=ALU.add)
+            prod[u] = [[sm[:, 0, :]], [sm[:, 1, :]]]
+
         def back(u, ips=(0, 1)):
             for ip in ips:
                 tr = pst.tile([P, 2, 2, P], F32, name="tr")
@@ -303,7 +311,7 @@ def tile_multiscaleretention_pa_kernel(tc, x, w_bytes, w_scale, b, out):
                     for e in range(2):
                         for q, part in enumerate(prod[u][e]):
                             nc.tensor.matmul(out=tr[:, i2, e, :], lhsT=part[:, blk], rhs=ident[:], is_transpose=True,
-                                             start=(q == 0), stop=(q == 1))
+                                             start=(q == 0), stop=(q == len(prod[u][e]) - 1))
                 trb[(u, ip)] = tr
 
         def leave(u, engs="SS", stores=1):
@@ -402,7 +410,7 @@ def tile_multiscaleretention_pa_kernel(tc, x, w_bytes, w_scale, b, out):
         products(1)
         leave(0)
 
-        for u in range(2, 2 * H):
+        for u in range(2, 2 * H - 2):
             h, half = u // 2, u % 2
             if half == 1:
                 back(u - 1)
@@ -422,4 +430,12 @@ def tile_multiscaleretention_pa_kernel(tc, x, w_bytes, w_scale, b, out):
                 w_int(k, 2 - 2 * half, "G")
             products(u, 2 if u == 2 * H - 1 else 1)
             leave(u - 1)
-        leave(2 * H - 1, "SV", 2)
+        add(13)
+        mx(15)
+        back(13)
+        products(14)
+        leave(13, "SS", 2)
+        back(14)
+        products(15, 2)
+        leave(14, "SS", 2)
+        leave(15, "SV", 2)

@@ -39,7 +39,7 @@ def tile_multiscaleretention_pa_kernel(tc, x, w_bytes, w_scale, b, out):
         epi = ctx.enter_context(tc.tile_pool(name="epi", bufs=2))
         outp = ctx.enter_context(tc.tile_pool(name="outp", bufs=3))
         tokp = ctx.enter_context(tc.tile_pool(name="tokp", bufs=3))
-        sump = ctx.enter_context(tc.tile_pool(name="sump", bufs=1))
+        sump = ctx.enter_context(tc.tile_pool(name="sump", bufs=2))
         psa = ctx.enter_context(tc.psum_pool(name="psa", bufs=2))
         pst = ctx.enter_context(tc.psum_pool(name="pst", bufs=4))
         ctx.enter_context(tc.manual_schedule())
@@ -269,17 +269,16 @@ def tile_multiscaleretention_pa_kernel(tc, x, w_bytes, w_scale, b, out):
         def banks(u):
             acc[u] = [psa.tile([P, 512], F32, name="acc%d" % e) for e in range(2)]
 
-        def mx(u):
+        def mx(u, by_g=False):
             h, nh = u // 2, u % 2
             if u not in acc:
                 banks(u)
-            for e in range(2):
-                a = acc[u][e]
-                for g in range(4):
-                    wcols = slice(256 * g + 128 * e, 256 * g + 128 * (e + 1))
-                    nc.tensor.matmul_mx(out=a[:], lhsT=wc[h][:, wcols].bitcast(FP8X4), lhsT_scale=ws[h][:, wcols],
-                                        rhs=xc[nh][:, g, :].bitcast(FP8X4), rhs_scale=xs[nh][:, g, :],
-                                        start=(g == 0), stop=(g == 3))
+            order = [(e, g) for g in range(4) for e in range(2)] if by_g else [(e, g) for e in range(2) for g in range(4)]
+            for e, g in order:
+                wcols = slice(256 * g + 128 * e, 256 * g + 128 * (e + 1))
+                nc.tensor.matmul_mx(out=acc[u][e][:], lhsT=wc[h][:, wcols].bitcast(FP8X4), lhsT_scale=ws[h][:, wcols],
+                                    rhs=xc[nh][:, g, :].bitcast(FP8X4), rhs_scale=xs[nh][:, g, :],
+                                    start=(g == 0), stop=(g == 3))
 
         def products(u, pieces=1):
             h, nh = u // 2, u % 2
@@ -298,10 +297,12 @@ def tile_multiscaleretention_pa_kernel(tc, x, w_bytes, w_scale, b, out):
                 if pieces > 1:
                     back(u, (piece,))
 
-        def add(u):
+        def add(u, es=(0, 1)):
             sm = sump.tile([P, 2, 512], F32, name="sm")
-            nc.gpsimd.tensor_tensor(out=sm[:], in0=pair[u][0][:], in1=pair[u][1][:], op=ALU.add)
-            prod[u] = [[sm[:, 0, :]], [sm[:, 1, :]]]
+            e0, e1 = es[0], es[-1] + 1
+            nc.gpsimd.tensor_tensor(out=sm[:, e0:e1, :], in0=pair[u][0][:, e0:e1, :], in1=pair[u][1][:, e0:e1, :], op=ALU.add)
+            for e in es:
+                prod[u][e] = [sm[:, e, :]]
 
         def back(u, ips=(0, 1)):
             for ip in ips:
@@ -368,11 +369,12 @@ def tile_multiscaleretention_pa_kernel(tc, x, w_bytes, w_scale, b, out):
         x_q(0, 1)
         x_q(0, 2)
         x_q(0, 3)
-        mx(0)
+        mx(0, True)
+        negate(0, 256, 512, "V")
         nc.vector.tensor_copy(out=bias[:], in_=b16[:].rearrange("p h e -> p (h e)"))
+        rotate_a(512, 2)
         w_deq(1, 0)
         w_deq(1, 1)
-        negate(0, 256, 512, "S")
         w_deq(1, 2)
         w_deq(1, 3)
         for g in range(4):
@@ -393,16 +395,15 @@ def tile_multiscaleretention_pa_kernel(tc, x, w_bytes, w_scale, b, out):
             x_ev(1, g, 1, "S")
         for g in range(4):
             x_q(1, g)
-        mx(1)
-        rotate_a(512, 2)
+        mx(1, True)
         w_q(1, 0, 4)
         rotate_b(512, 2)
         back(0)
         mx(2)
         w_deq(2, 0)
         w_deq(2, 1)
-        negate(1, 0, 512, "S")
         w_deq(2, 2)
+        negate(1, 0, 512, "S")
         w_deq(2, 3)
         w_int(2, 1, "V")
         new_token()
@@ -434,6 +435,7 @@ def tile_multiscaleretention_pa_kernel(tc, x, w_bytes, w_scale, b, out):
         mx(15)
         back(13)
         products(14)
+        add(14, (0,))
         leave(13, "SS", 2)
         back(14)
         products(15, 2)

@@ -44,6 +44,8 @@ def tile_multiscaleretention_pa_kernel(tc, x, w_bytes, w_scale, b, out):
         pst = ctx.enter_context(tc.psum_pool(name="pst", bufs=4))
         ctx.enter_context(tc.manual_schedule())
 
+        wsc = const.tile([P, 4, 4], F32, name="wsc")
+        nc.scalar.dma_start(out=wsc[:], in_=w_scale.rearrange("(g p t) o -> p g (t o)", p=P, t=4))
         zero = const.tile([P, 1], F32, name="zero")
         nc.vector.memset(zero[:], 0.0)
         warm = const.tile([P, 1], F32, name="warm")
@@ -52,8 +54,6 @@ def tile_multiscaleretention_pa_kernel(tc, x, w_bytes, w_scale, b, out):
         nc.vector.tensor_scalar(out=halfpi[:], in0=zero[:], scalar1=1.0, scalar2=PI / 2.0,
                                 op0=ALU.mult, op1=ALU.add)
 
-        wsc = const.tile([P, 4, 4], F32, name="wsc")
-        nc.scalar.dma_start(out=wsc[:], in_=w_scale.rearrange("(g p t) o -> p g (t o)", p=P, t=4))
         b16 = const.tile([P, H, 2], BF16, name="b16")
 
         wsrc = {}
@@ -77,13 +77,13 @@ def tile_multiscaleretention_pa_kernel(tc, x, w_bytes, w_scale, b, out):
                 nc.sync.dma_start(out=xt[:, 2 * ip:2 * ip + 2, :], in_=xv[:, 2 * ip:2 * ip + 2, :])
             x_sb.append(xt)
 
-        load_w(0, 2)
+        load_w(0, 1)
         load_x(0)
+        load_w(1, 1)
         nc.sync.dma_start(out=b16[:], in_=b.rearrange("(h j e) -> j h e", h=H, e=2))
         load_x(1)
         load_w(2, 2)
-        load_w(4, 2)
-        load_w(6, 2)
+        load_w(4, 4)
 
         jcol = const.tile([P, 1], I32, name="jcol")
         nc.gpsimd.iota(jcol[:], pattern=[[0, 1]], base=0, channel_multiplier=1)

@@ -39,7 +39,7 @@ def tile_multiscaleretention_pa_kernel(tc, x, w_bytes, w_scale, b, out):
         epi = ctx.enter_context(tc.tile_pool(name="epi", bufs=2))
         outp = ctx.enter_context(tc.tile_pool(name="outp", bufs=3))
         tokp = ctx.enter_context(tc.tile_pool(name="tokp", bufs=3))
-        sump = ctx.enter_context(tc.tile_pool(name="sump", bufs=2))
+        sump = ctx.enter_context(tc.tile_pool(name="sump", bufs=4))
         psa = ctx.enter_context(tc.psum_pool(name="psa", bufs=2))
         pst = ctx.enter_context(tc.psum_pool(name="pst", bufs=4))
         ctx.enter_context(tc.manual_schedule())
@@ -297,6 +297,13 @@ def tile_multiscaleretention_pa_kernel(tc, x, w_bytes, w_scale, b, out):
                 if pieces > 1:
                     back(u, (piece,))
 
+        def addv(u, es=(0,)):
+            sm = sump.tile([P, 2, 512], F32, name="sm")
+            e0, e1 = es[0], es[-1] + 1
+            nc.vector.tensor_tensor(out=sm[:, e0:e1, :], in0=pair[u][0][:, e0:e1, :], in1=pair[u][1][:, e0:e1, :], op=ALU.add)
+            for e in es:
+                prod[u][e] = [sm[:, e, :]]
+
         def add(u, es=(0, 1)):
             sm = sump.tile([P, 2, 512], F32, name="sm")
             e0, e1 = es[0], es[-1] + 1
@@ -395,10 +402,10 @@ def tile_multiscaleretention_pa_kernel(tc, x, w_bytes, w_scale, b, out):
             x_ev(1, g, 1, "S")
         for g in range(4):
             x_q(1, g)
+        back(0)
         mx(1, True)
         w_q(1, 0, 4)
         rotate_b(512, 2)
-        back(0)
         mx(2)
         w_deq(2, 0)
         w_deq(2, 1)
@@ -419,16 +426,18 @@ def tile_multiscaleretention_pa_kernel(tc, x, w_bytes, w_scale, b, out):
                     w_q(h + 1, 0, 4)
             if u + 1 < 2 * H:
                 mx(u + 1)
-            if half == 0:
-                back(u - 1)
             if h + 2 < H:
                 w_deq(h + 2, 2 * half)
                 w_deq(h + 2, 2 * half + 1)
             k = h + 1 + half
             if k < H:
                 w_int(k, 3 - 2 * half, "V")
+                if half == 0 and h % 2 == 0:
+                    addv(u - 1)
                 new_token()
                 w_int(k, 2 - 2 * half, "G")
+            if half == 0:
+                back(u - 1)
             products(u, 2 if u == 2 * H - 1 else 1)
             leave(u - 1)
         add(13)

@@ -36,7 +36,7 @@ def tile_multiscaleretention_pa_kernel(tc, x, w_bytes, w_scale, b, out):
         wprep = ctx.enter_context(tc.tile_pool(name="wprep", bufs=2))
         wq = ctx.enter_context(tc.tile_pool(name="wq", bufs=3))
         xprep = ctx.enter_context(tc.tile_pool(name="xprep", bufs=4))
-        epi = ctx.enter_context(tc.tile_pool(name="epi", bufs=2))
+        epi = ctx.enter_context(tc.tile_pool(name="epi", bufs=3))
         outp = ctx.enter_context(tc.tile_pool(name="outp", bufs=3))
         tokp = ctx.enter_context(tc.tile_pool(name="tokp", bufs=3))
         sump = ctx.enter_context(tc.tile_pool(name="sump", bufs=4))
@@ -286,16 +286,16 @@ def tile_multiscaleretention_pa_kernel(tc, x, w_bytes, w_scale, b, out):
             uo = epi.tile([P, 2, 512], F32, name="uo")
             prod[u] = [[ue[:, 0, :], uo[:, 0, :]], [uo[:, 1, :], ue[:, 1, :]]]
             pair[u] = (ue, uo)
-            width = 512 // pieces
-            for piece in range(pieces):
-                c = slice(width * piece, width * (piece + 1))
-                for dst, e, seg in ((ue, 0, 1), (uo, 1, 0)):
+            for dst, e, seg, n in ((ue, 0, 1, 1), (uo, 1, 0, pieces)):
+                width = 512 // n
+                for piece in range(n):
+                    c = slice(width * piece, width * (piece + 1))
                     nc.vector.scalar_tensor_tensor(out=dst[:, :, c],
                                                    in0=acc[u][e][:, c].unsqueeze(1).to_broadcast([P, 2, width]),
                                                    scalar=bias[:, 2 * h + e:2 * h + e + 1], in1=tab3[:, nh, seg:seg + 2, c],
                                                    op0=ALU.add, op1=ALU.mult)
-                if pieces > 1:
-                    back(u, (piece,))
+                    if n > 1:
+                        back(u, (piece,))
 
         def addv(u, es=(0,)):
             sm = sump.tile([P, 2, 512], F32, name="sm")
@@ -304,9 +304,11 @@ def tile_multiscaleretention_pa_kernel(tc, x, w_bytes, w_scale, b, out):
             for e in es:
                 prod[u][e] = [sm[:, e, :]]
 
-        def add(u, es=(0, 1)):
+        def add(u, es=(0, 1), guard=False):
             sm = sump.tile([P, 2, 512], F32, name="sm")
             e0, e1 = es[0], es[-1] + 1
+            if guard:
+                nc.vector.memset(sm[:, e0, 0:1], 0.0)
             nc.gpsimd.tensor_tensor(out=sm[:, e0:e1, :], in0=pair[u][0][:, e0:e1, :], in1=pair[u][1][:, e0:e1, :], op=ALU.add)
             for e in es:
                 prod[u][e] = [sm[:, e, :]]
@@ -418,7 +420,7 @@ def tile_multiscaleretention_pa_kernel(tc, x, w_bytes, w_scale, b, out):
         products(1)
         leave(0)
 
-        for u in range(2, 2 * H - 2):
+        for u in range(2, 2 * H - 4):
             h, half = u // 2, u % 2
             if half == 1:
                 back(u - 1)
@@ -440,11 +442,24 @@ def tile_multiscaleretention_pa_kernel(tc, x, w_bytes, w_scale, b, out):
                 back(u - 1)
             products(u, 2 if u == 2 * H - 1 else 1)
             leave(u - 1)
+        mx(13)
+        w_int(7, 3, "S")
+        new_token()
+        w_int(7, 2, "G")
+        back(11)
+        products(12)
+        leave(11)
+        w_q(7, 0, 4)
+        mx(14)
+        add(12, (0, 1), True)
+        products(13)
         add(13)
+        back(12)
+        leave(12, "SS", 2)
         mx(15)
-        back(13)
         products(14)
         add(14, (0,))
+        back(13)
         leave(13, "SS", 2)
         back(14)
         products(15, 2)

from contextlib import ExitStack

import concourse.mybir as mybir
from concourse.masks import make_identity

F32 = mybir.dt.float32
BF16 = mybir.dt.bfloat16
I32 = mybir.dt.int32
U32 = mybir.dt.uint32
U8 = mybir.dt.uint8
FP8 = mybir.dt.float8_e4m3fn
FP8X4 = mybir.dt.float8_e4m3fn_x4
ALU = mybir.AluOpType
ACT = mybir.ActivationFunctionType

P = 128
N_TOK = 1024
E = 2048
H = 8
FLOPS = 2 * N_TOK * E * E

Q = 10000.0 ** (-1.0 / 127.0)
PI = 3.141592653589793
TWO_PI = 2.0 * PI
C1 = 51472.0 / 8192.0
C2 = TWO_PI - C1


def tile_multiscaleretention_pa_kernel(tc, x, w_bytes, w_scale, b, out):
    nc = tc.nc
    with ExitStack() as ctx:
        const = ctx.enter_context(tc.tile_pool(name="const", bufs=1))
        xin = ctx.enter_context(tc.tile_pool(name="xin", bufs=1))
        wbp = ctx.enter_context(tc.tile_pool(name="wbp", bufs=1))
        scr = ctx.enter_context(tc.tile_pool(name="scr", bufs=1))
        wprep = ctx.enter_context(tc.tile_pool(name="wprep", bufs=2))
        wq = ctx.enter_context(tc.tile_pool(name="wq", bufs=3))
        xprep = ctx.enter_context(tc.tile_pool(name="xprep", bufs=4))
        epi = ctx.enter_context(tc.tile_pool(name="epi", bufs=3))
        outp = ctx.enter_context(tc.tile_pool(name="outp", bufs=3))
        tokp = ctx.enter_context(tc.tile_pool(name="tokp", bufs=3))
        sump = ctx.enter_context(tc.tile_pool(name="sump", bufs=4))
        psa = ctx.enter_context(tc.psum_pool(name="psa", bufs=2))
        pst = ctx.enter_context(tc.psum_pool(name="pst", bufs=4))
        ctx.enter_context(tc.manual_schedule())

        wsc = const.tile([P, 4, 4], F32, name="wsc")
        nc.scalar.dma_start(out=wsc[:], in_=w_scale.rearrange("(g p t) o -> p g (t o)", p=P, t=4))
        zero = const.tile([P, 1], F32, name="zero")
        nc.vector.memset(zero[:], 0.0)
        warm = const.tile([P, 1], F32, name="warm")
        nc.scalar.activation(out=warm[:], in_=zero[:], func=ACT.Sin)
        halfpi = const.tile([P, 1], F32, name="halfpi")
        nc.vector.tensor_scalar(out=halfpi[:], in0=zero[:], scalar1=1.0, scalar2=PI / 2.0,
                                op0=ALU.mult, op1=ALU.add)

        b16 = const.tile([P, H, 2], BF16, name="b16")

        wsrc = {}

        def load_w(h0, heads):
            width = 256 * heads
            for g in range(4):
                wbt = wbp.tile([P, 4, width], U8, name="wb%d_%d" % (h0, g))
                nc.sync.dma_start(
                    out=wbt[:],
                    in_=w_bytes[512 * g:512 * (g + 1), 256 * h0:256 * h0 + width].rearrange("(p t) n -> p t n", t=4))
                for hh in range(heads):
                    wsrc[(h0 + hh, g)] = (wbt, 256 * hh)

        x_sb = []

        def load_x(nh):
            xt = xin.tile([P, 4, 2048], BF16, name="xin%d" % nh)
            xv = x[0, 512 * nh:512 * (nh + 1), :].rearrange("(p i) k -> p i k", i=4)
            for ip in range(2):
                nc.sync.dma_start(out=xt[:, 2 * ip:2 * ip + 2, :], in_=xv[:, 2 * ip:2 * ip + 2, :])
            x_sb.append(xt)

        load_w(0, 1)
        load_x(0)
        load_w(1, 1)
        nc.sync.dma_start(out=b16[:], in_=b.rearrange("(h j e) -> j h e", h=H, e=2))
        load_x(1)
        load_w(2, 2)
        load_w(4, 4)

        jcol = const.tile([P, 1], I32, name="jcol")
        nc.gpsimd.iota(jcol[:], pattern=[[0, 1]], base=0, channel_multiplier=1)
        nfb = const.tile([P, 132], F32, name="nfb")
        nc.gpsimd.iota(nfb[:, 0:128], pattern=[[4, 128]], base=0, channel_multiplier=0,
                       allow_small_or_imprecise_dtypes=True)
        nc.gpsimd.iota(nfb[:, 128:132], pattern=[[511, 2], [1, 2]], base=1, channel_multiplier=0,
                       allow_small_or_imprecise_dtypes=True)
        ident = const.tile([P, P], F32, name="ident")
        make_identity(nc, ident[:])

        bit = const.tile([P, 7], I32, name="bit")
        for bb in range(7):
            nc.vector.tensor_scalar(out=bit[:, bb:bb + 1], in0=jcol[:], scalar1=bb, scalar2=1,
                                    op0=ALU.logical_shift_right, op1=ALU.bitwise_and)
        fac = const.tile([P, 7], F32, name="fac")
        for bb in range(7):
            nc.vector.tensor_scalar(out=fac[:, bb:bb + 1], in0=bit[:, bb:bb + 1], scalar1=0.0, scalar2=Q ** (2 ** bb),
                                    op0=ALU.is_equal, op1=ALU.max)
        pr3 = const.tile([P, 3], F32, name="pr3")
        nc.vector.tensor_tensor(out=pr3[:], in0=fac[:, 0:3], in1=fac[:, 3:6], op=ALU.mult)
        pr2 = const.tile([P, 2], F32, name="pr2")
        nc.vector.tensor_tensor(out=pr2[:, 0:1], in0=pr3[:, 0:1], in1=pr3[:, 1:2], op=ALU.mult)
        nc.vector.tensor_tensor(out=pr2[:, 1:2], in0=pr3[:, 2:3], in1=fac[:, 6:7], op=ALU.mult)
        theta = const.tile([P, 1], F32, name="theta")
        nc.vector.tensor_tensor(out=theta[:], in0=pr2[:, 0:1], in1=pr2[:, 1:2], op=ALU.mult)

        tab3 = const.tile([P, 2, 3, 512], F32, name="tab3")

        cx = const.tile([P, 4], F32, name="cx")
        sx = const.tile([P, 4], F32, name="sx")
        sn = scr.tile([P, 132], F32, name="sn")
        cs = scr.tile([P, 132], F32, name="cs")

        kk = scr.tile([P, 132], I32, name="kk")
        kc1 = scr.tile([P, 132], F32, name="kc1")
        r1 = scr.tile([P, 132], F32, name="r1")
        rr = scr.tile([P, 132], F32, name="rr")
        psi = scr.tile([P, 132], F32, name="psi")
        ab = scr.tile([P, 132], F32, name="ab")
        tmp = scr.tile([P, 132], F32, name="tmp")

        def arg_step(step):
            if step == 0:
                nc.vector.tensor_scalar(out=kk[:], in0=nfb[:], scalar1=theta[:, 0:1], scalar2=1.0 / TWO_PI,
                                        op0=ALU.mult, op1=ALU.mult)
            elif step == 1:
                nc.vector.tensor_scalar(out=kc1[:], in0=kk[:], scalar1=C1, scalar2=None, op0=ALU.mult)
            elif step == 2:
                nc.vector.scalar_tensor_tensor(out=r1[:], in0=nfb[:], scalar=theta[:, 0:1], in1=kc1[:],
                                               op0=ALU.mult, op1=ALU.subtract)
            elif step == 3:
                nc.vector.scalar_tensor_tensor(out=rr[:], in0=kk[:], scalar=-C2, in1=r1[:],
                                               op0=ALU.mult, op1=ALU.add)
            elif step == 4:
                nc.vector.tensor_scalar(out=psi[:], in0=rr[:], scalar1=0.5, scalar2=-PI / 4.0,
                                        op0=ALU.mult, op1=ALU.add)
            else:
                nc.vector.scalar_tensor_tensor(out=ab[:], in0=psi[:], scalar=-1.0, in1=psi[:],
                                               op0=ALU.mult, op1=ALU.max)

        def base_sines():
            nc.scalar.activation(out=sn[:], in_=psi[:], func=ACT.Sin)
            nc.scalar.activation(out=cs[:], in_=ab[:], func=ACT.Sin, scale=-1.0, bias=halfpi[:, 0:1])

        def base_step(step):
            if step == 0:
                nc.vector.scalar_tensor_tensor(out=tmp[:], in0=sn[:], scalar=-2.0, in1=sn[:],
                                               op0=ALU.mult, op1=ALU.mult)
            elif step == 1:
                nc.vector.scalar_tensor_tensor(out=cx[:], in0=sn[:, 128:132], scalar=-2.0, in1=cs[:, 128:132],
                                               op0=ALU.mult, op1=ALU.mult)
                nc.vector.scalar_tensor_tensor(out=tab3[:, 0, 1, 0:128], in0=sn[:, 0:128], scalar=-2.0, in1=cs[:, 0:128],
                                               op0=ALU.mult, op1=ALU.mult)
            else:
                nc.vector.tensor_scalar(out=sx[:], in0=tmp[:, 128:132], scalar1=1.0, scalar2=1.0,
                                        op0=ALU.mult, op1=ALU.add)
                nc.vector.tensor_scalar(out=tab3[:, 0, 2, 0:128], in0=tmp[:, 0:128], scalar1=1.0, scalar2=1.0,
                                        op0=ALU.mult, op1=ALU.add)
                nc.vector.tensor_scalar(out=tab3[:, 0, 0, 0:128], in0=tmp[:, 0:128], scalar1=-1.0, scalar2=-1.0,
                                        op0=ALU.mult, op1=ALU.add)

        rot = {}

        def rotate_a(width, k):
            t1 = scr.tile([P, 2, 512], F32, name="rot")
            nc.vector.tensor_scalar(out=t1[:, :, 0:width], in0=tab3[:, 0, 0:2, 0:width], scalar1=sx[:, k:k + 1],
                                    scalar2=None, op0=ALU.mult)
            rot[0] = t1

        def rotate_b(width, k):
            dst = tab3[:, 1, 1:3, :] if width == 512 else tab3[:, 0, 1:3, width:2 * width]
            nc.vector.scalar_tensor_tensor(out=dst, in0=tab3[:, 0, 1:3, 0:width], scalar=cx[:, k:k + 1],
                                           in1=rot[0][:, :, 0:width], op0=ALU.mult, op1=ALU.add)

        def negate(nh, c0, c1, eng):
            if eng == "S":
                nc.scalar.activation(out=tab3[:, nh, 0, c0:c1], in_=tab3[:, nh, 2, c0:c1], func=ACT.Copy, scale=-1.0)
            else:
                nc.vector.tensor_scalar(out=tab3[:, nh, 0, c0:c1], in0=tab3[:, nh, 2, c0:c1], scalar1=-1.0, scalar2=None,
                                        op0=ALU.mult)

        xc = [const.tile([P, 4, 512], U32, name="xc%d" % nh, align_bytes=64) for nh in range(2)]
        xs = [const.tile([P, 4, 512], U8, name="xs%d" % nh, align_bytes=64) for nh in range(2)]
        xg = {}
        xbank = {}

        def x_tr(nh, g, ip):
            xt = pst.tile([P, 2, 2, P], F32, name="tr")
            for i2 in range(2):
                words = x_sb[nh][:, 2 * ip + i2, :].bitcast(F32)
                for u in range(2):
                    nc.tensor.transpose(xt[:, i2, u, :], words[:, 256 * g + u:256 * (g + 1):2], ident[:])
            xbank[(nh, g, ip)] = xt

        def x_ev(nh, g, ip, eng):
            if (nh, g) not in xg:
                xg[(nh, g)] = xprep.tile([P, 2048], BF16, name="xg", align_bytes=64)
            xgw = xg[(nh, g)][:].bitcast(F32)
            dst = xgw[:, 512 * ip:512 * (ip + 1)].rearrange("p (i r u) -> p i r u", i=2, u=2)
            src = xbank[(nh, g, ip)][:].rearrange("p i u r -> p i r u")
            if eng == "V":
                nc.vector.tensor_copy(out=dst, in_=src)
            else:
                nc.scalar.copy(out=dst, in_=src)

        def x_q(nh, g):
            nc.vector.quantize_mx(out=xc[nh][:, g, :].bitcast(FP8X4), scales=xs[nh][:, g, :], in_=xg[(nh, g)][:])

        deq = {}
        grp = {}
        wc = {}
        ws = {}

        def w_deq(h, g, eng="S"):
            if h not in deq:
                deq[h] = wprep.tile([P, 16, 256], BF16, name="deq")
            wbt, c0 = wsrc[(h, g)]
            for t in range(4):
                if eng == "S":
                    nc.scalar.activation(out=deq[h][:, 4 * g + t, :], in_=wbt[:, t, c0:c0 + 256].bitcast(FP8),
                                         func=ACT.Copy, scale=wsc[:, g, t:t + 1])
                else:
                    nc.vector.tensor_scalar(out=deq[h][:, 4 * g + t, :], in0=wbt[:, t, c0:c0 + 256].bitcast(FP8),
                                            scalar1=wsc[:, g, t:t + 1], scalar2=None, op0=ALU.mult)

        def w_int(h, g, eng):
            if h not in grp:
                grp[h] = wprep.tile([P, 4096], BF16, name="grp", align_bytes=64)
            dst = grp[h][:, 1024 * g:1024 * (g + 1)].rearrange("p (e j t) -> p e j t", e=2, t=4)
            src = deq[h][:, 4 * g:4 * g + 4, :].rearrange("p t (j e) -> p e j t", e=2)
            if eng == "S":
                nc.scalar.copy(out=dst, in_=src)
            elif eng == "V":
                nc.vector.tensor_copy(
                    out=grp[h][:, 1024 * g:1024 * (g + 1)].rearrange("p (e c i t) -> p e c t i", e=2, i=4, t=4),
                    in_=deq[h][:, 4 * g:4 * g + 4, :].rearrange("p t (c i e) -> p e c t i", i=4, e=2))
            else:
                nc.gpsimd.tensor_scalar(out=dst, in0=src, scalar1=token[0][:, 0:1], scalar2=0.0,
                                        op0=ALU.mult, op1=ALU.add)

        token = [None]

        def new_token():
            tok = tokp.tile([P, 1], F32, name="tok")
            nc.vector.tensor_scalar(out=tok[:], in0=zero[:], scalar1=1.0, scalar2=1.0, op0=ALU.mult, op1=ALU.add)
            token[0] = tok

        def w_q(h, g0, ng):
            if h not in wc:
                wc[h] = wq.tile([P, 1024], U32, name="wcod", align_bytes=64)
                ws[h] = wq.tile([P, 1024], U8, name="wsca", align_bytes=64)
            nc.vector.quantize_mx(out=wc[h][:, 256 * g0:256 * (g0 + ng)].bitcast(FP8X4),
                                  scales=ws[h][:, 256 * g0:256 * (g0 + ng)],
                                  in_=grp[h][:, 1024 * g0:1024 * (g0 + ng)])

        acc = {}
        prod = {}
        pair = {}
        trb = {}
        bias = const.tile([P, 2 * H], F32, name="bias")

        def banks(u):
            acc[u] = [psa.tile([P, 512], F32, name="acc%d" % e) for e in range(2)]

        def mx(u, by_g=False):
            h, nh = u // 2, u % 2
            if u not in acc:
                banks(u)
            order = [(e, g) for g in range(4) for e in range(2)] if by_g else [(e, g) for e in range(2) for g in range(4)]
            for e, g in order:
                wcols = slice(256 * g + 128 * e, 256 * g + 128 * (e + 1))
                nc.tensor.matmul_mx(out=acc[u][e][:], lhsT=wc[h][:, wcols].bitcast(FP8X4), lhsT_scale=ws[h][:, wcols],
                                    rhs=xc[nh][:, g, :].bitcast(FP8X4), rhs_scale=xs[nh][:, g, :],
                                    start=(g == 0), stop=(g == 3))

        def products(u, pieces=1):
            h, nh = u // 2, u % 2
            ue = epi.tile([P, 2, 512], F32, name="ue")
            uo = epi.tile([P, 2, 512], F32, name="uo")
            prod[u] = [[ue[:, 0, :], uo[:, 0, :]], [uo[:, 1, :], ue[:, 1, :]]]
            pair[u] = (ue, uo)
            for dst, e, seg, n in ((ue, 0, 1, 1), (uo, 1, 0, pieces)):
                width = 512 // n
                for piece in range(n):
                    c = slice(width * piece, width * (piece + 1))
                    nc.vector.scalar_tensor_tensor(out=dst[:, :, c],
                                                   in0=acc[u][e][:, c].unsqueeze(1).to_broadcast([P, 2, width]),
                                                   scalar=bias[:, 2 * h + e:2 * h + e + 1], in1=tab3[:, nh, seg:seg + 2, c],
                                                   op0=ALU.add, op1=ALU.mult)
                    if n > 1:
                        back(u, (piece,))

        def addv(u, es=(0,)):
            sm = sump.tile([P, 2, 512], F32, name="sm")
            e0, e1 = es[0], es[-1] + 1
            nc.vector.tensor_tensor(out=sm[:, e0:e1, :], in0=pair[u][0][:, e0:e1, :], in1=pair[u][1][:, e0:e1, :], op=ALU.add)
            for e in es:
                prod[u][e] = [sm[:, e, :]]

        def add(u, es=(0, 1), guard=False):
            sm = sump.tile([P, 2, 512], F32, name="sm")
            e0, e1 = es[0], es[-1] + 1
            if guard:
                nc.vector.memset(sm[:, e0, 0:1], 0.0)
            nc.gpsimd.tensor_tensor(out=sm[:, e0:e1, :], in0=pair[u][0][:, e0:e1, :], in1=pair[u][1][:, e0:e1, :], op=ALU.add)
            for e in es:
                prod[u][e] = [sm[:, e, :]]

        def back(u, ips=(0, 1)):
            for ip in ips:
                tr = pst.tile([P, 2, 2, P], F32, name="tr")
                for i2 in range(2):
                    blk = slice(128 * (2 * ip + i2), 128 * (2 * ip + i2 + 1))
                    for e in range(2):
                        for q, part in enumerate(prod[u][e]):
                            nc.tensor.matmul(out=tr[:, i2, e, :], lhsT=part[:, blk], rhs=ident[:], is_transpose=True,
                                             start=(q == 0), stop=(q == len(prod[u][e]) - 1))
                trb[(u, ip)] = tr

        def leave(u, engs="SS", stores=1):
            h, nh = u // 2, u % 2
            osb = outp.tile([P, 4, 256], F32, name="osb")
            dram = out[0, h, 512 * nh:512 * (nh + 1), :].rearrange("(p i) d -> p i d", i=4)
            for ip in range(2):
                dst = osb[:, 2 * ip:2 * ip + 2, :].rearrange("p i (j e) -> p i j e", e=2)
                src = trb[(u, ip)][:].rearrange("p i e j -> p i j e")
                if engs[ip] == "S":
                    nc.scalar.copy(out=dst, in_=src)
                else:
                    nc.vector.tensor_copy(out=dst, in_=src)
                if stores == 2:
                    nc.sync.dma_start(out=dram[:, 2 * ip:2 * ip + 2, :], in_=osb[:, 2 * ip:2 * ip + 2, :])
            if stores == 1:
                nc.sync.dma_start(out=dram, in_=osb[:])

        arg_step(0)
        arg_step(1)
        w_deq(0, 0, "V")
        w_deq(0, 1)
        w_deq(0, 2)
        w_int(0, 0, "V")
        arg_step(2)
        arg_step(3)
        w_int(0, 1, "V")
        arg_step(4)
        arg_step(5)
        base_sines()
        w_deq(0, 3)
        w_int(0, 2, "V")
        for g in range(4):
            x_tr(0, g, 0)
        base_step(0)
        x_ev(0, 0, 0, "S")
        base_step(1)
        base_step(2)
        x_ev(0, 1, 0, "S")
        x_ev(0, 2, 0, "S")
        x_ev(0, 3, 0, "S")
        for g in range(4):
            x_tr(0, g, 1)
        w_int(0, 3, "V")
        rotate_a(128, 0)
        rotate_b(128, 0)
        w_q(0, 0, 4)
        negate(0, 128, 256, "V")
        for g in range(4):
            x_ev(0, g, 1, "S")
        rotate_a(256, 1)
        x_q(0, 0)
        rotate_b(256, 1)
        x_q(0, 1)
        x_q(0, 2)
        x_q(0, 3)
        mx(0, True)
        negate(0, 256, 512, "V")
        nc.vector.tensor_copy(out=bias[:], in_=b16[:].rearrange("p h e -> p (h e)"))
        rotate_a(512, 2)
        w_deq(1, 0)
        w_deq(1, 1)
        w_deq(1, 2)
        w_deq(1, 3)
        for g in range(4):
            x_tr(1, g, 0)
        new_token()
        w_int(1, 0, "G")
        w_int(1, 1, "G")
        products(0)
        x_ev(1, 0, 0, "V")
        x_ev(1, 1, 0, "V")
        x_ev(1, 2, 0, "S")
        x_ev(1, 3, 0, "S")
        for g in range(4):
            x_tr(1, g, 1)
        w_int(1, 2, "V")
        w_int(1, 3, "V")
        for g in range(4):
            x_ev(1, g, 1, "S")
        for g in range(4):
            x_q(1, g)
        back(0)
        mx(1, True)
        w_q(1, 0, 4)
        rotate_b(512, 2)
        mx(2)
        w_deq(2, 0)
        w_deq(2, 1)
        w_deq(2, 2)
        negate(1, 0, 512, "S")
        w_deq(2, 3)
        w_int(2, 1, "V")
        new_token()
        w_int(2, 0, "G")
        products(1)
        leave(0)

        for u in range(2, 2 * H - 4):
            h, half = u // 2, u % 2
            if half == 1:
                back(u - 1)
                if h + 1 < H:
                    w_q(h + 1, 0, 4)
            if u + 1 < 2 * H:
                mx(u + 1)
            if h + 2 < H:
                w_deq(h + 2, 2 * half)
                w_deq(h + 2, 2 * half + 1)
            k = h + 1 + half
            if k < H:
                w_int(k, 3 - 2 * half, "V")
                if half == 0 and h % 2 == 0:
                    addv(u - 1)
                new_token()
                w_int(k, 2 - 2 * half, "G")
            if half == 0:
                back(u - 1)
            products(u, 2 if u == 2 * H - 1 else 1)
            leave(u - 1)
        mx(13)
        w_int(7, 3, "S")
        new_token()
        w_int(7, 2, "G")
        back(11)
        products(12)
        leave(11)
        w_q(7, 0, 4)
        mx(14)
        add(12, (0, 1), True)
        products(13)
        add(13)
        back(12)
        leave(12, "SS", 2)
        mx(15)
        products(14)
        add(14, (0,))
        back(13)
        leave(13, "SS", 2)
        back(14)
        products(15, 2)
        leave(14, "SS", 2)
        leave(15, "SV", 2)
